import numpy as np
import ml_dtypes


def mxq(x, axis, fmt="e4m3"):
    dtype, down = {"e4m3": (ml_dtypes.float8_e4m3fn, 7), "e5m2": (ml_dtypes.float8_e5m2, 14)}[fmt]
    v = np.moveaxis(np.asarray(x, np.float32).astype(ml_dtypes.bfloat16).astype(np.float64), axis, -1)
    blocks = v.reshape(v.shape[:-1] + (-1, 32))
    amax = np.abs(blocks).max(-1, keepdims=True)
    byte = np.maximum(np.where(amax > 0, np.frexp(amax)[1] - 1 + 127, 0) - down, 1)
    scale = np.exp2(byte - 127.0)
    codes = (blocks / scale).astype(np.float32).astype(dtype).astype(np.float64)
    return np.moveaxis((codes * scale).reshape(v.shape), -1, axis)


WIDE = False


def mx_kscale(k):
    if not WIDE:
        return np.ones(k)
    levels = np.array([10, -10, 5, -5, 0])
    if k % 512:
        return np.exp2(np.random.permutation(np.resize(levels, k // 32))).repeat(32)
    a = np.empty((k // 512, 16))
    for p in range(k // 512):
        a[p, :8] = np.random.permutation(np.resize(levels, 8))
        for g in range(8):
            far = levels[np.abs(levels - a[p, g]) >= 10]
            a[p, g + 8] = far[np.random.randint(len(far))]
    return np.exp2(a.ravel()).repeat(32)


BF16 = ml_dtypes.bfloat16


def bf(x):
    return np.asarray(x, np.float32).astype(BF16)


def f64(x):
    return np.asarray(x).astype(np.float64)


B, G, DB, DR = 4096, 4, 512, 512


def mish(v):
    return v * np.tanh(np.log(1.0 + np.exp(v)))


def setup_inputs():
    s, t = mx_kscale(DR), mx_kscale(DB)
    return {"BB_feature": bf(np.random.standard_normal((B, G, DB)) * t),
            "RF_feature": bf(np.random.standard_normal((B, DR)) * s),
            "W_rfrf": bf(np.random.standard_normal((DR, DR)) / np.sqrt(DR) / s),
            "b_rfrf": bf(np.random.standard_normal(DR) * 0.5),
            "W_bbrf": bf(np.random.standard_normal((DR, DB)) * np.sqrt(G / DB) / t),
            "b_bbrf": bf(np.random.standard_normal(DR) * 0.5)}


def reference(BB_feature, RF_feature, W_rfrf, b_rfrf, W_bbrf, b_bbrf):
    BB_mean = np.mean(f64(BB_feature), axis=-2)
    RF_to_RF = mish((mxq(f64(RF_feature), 1, "e4m3") @ mxq(f64(W_rfrf), 1, "e4m3").T) + f64(b_rfrf))
    BB_to_RF = mish((mxq(BB_mean, 1, "e4m3") @ mxq(f64(W_bbrf), 1, "e4m3").T) + f64(b_bbrf))
    return RF_to_RF + BB_to_RF

@@ -1,0 +1,292 @@
+import concourse.mybir as mybir
+from concourse.masks import make_identity
+
+F32 = mybir.dt.float32
+BF16 = mybir.dt.bfloat16
+U32 = mybir.dt.uint32
+U8 = mybir.dt.uint8
+FP8X4 = mybir.dt.float8_e4m3fn_x4
+ACT = mybir.ActivationFunctionType
+ALU = mybir.AluOpType
+
+P = 128
+PACK = 4
+ROWS = 4096
+GROUPS = 4
+K = 512
+N_OUT = 512
+BLOCK = 512
+BLOCKS = ROWS // BLOCK
+SLABS = BLOCK // P
+CHUNKS = N_OUT // P
+BATCH = 2
+BATCHES = BLOCKS // BATCH
+STEPS = BATCH * CHUNKS
+LAG = 1
+BEHIND = 2
+AHEAD = 2
+RF = 0
+BB = 1
+BRANCHES = (RF, BB)
+PER_PIECE = P // GROUPS
+PIECES = P // PER_PIECE
+TENSOR_SLABS = 3
+TINY = 1e-18
+
+FLOPS = 2 * 2 * ROWS * K * N_OUT
+
+
+def tile_gnn_layer_pa_t_kernel(tc, BB_feature, RF_feature, W_rfrf, b_rfrf, W_bbrf, b_bbrf, out):
+    nc = tc.nc
+    bb_rows = BB_feature.rearrange("b g k -> (b g) k")
+
+    with tc.manual_schedule(), tc.tile_pool(name="const", bufs=1) as const, tc.tile_pool(
+        name="rf_loads", bufs=AHEAD + 3
+    ) as rf_loads, tc.tile_pool(name="bb_loads", bufs=AHEAD + 1) as bb_loads, tc.tile_pool(
+        name="sums", bufs=AHEAD + 2
+    ) as sums, tc.tile_pool(name="regroup", bufs=2) as regroup, tc.tile_pool(
+        name="stage", bufs=2 * STEPS
+    ) as stage, tc.tile_pool(
+        name="result", bufs=4
+    ) as result, tc.psum_pool(name="front", bufs=2) as front, tc.psum_pool(
+        name="products", bufs=4
+    ) as products, tc.psum_pool(name="back", bufs=2) as back:
+        ident_f32 = const.tile([P, P], F32)
+        make_identity(nc, ident_f32[:])
+        ident_bf16 = const.tile([P, P], BF16)
+        make_identity(nc, ident_bf16[:])
+        group_ones_f32 = const.tile([P, PER_PIECE], F32)
+        nc.vector.tensor_reduce(
+            out=group_ones_f32[:],
+            in_=ident_f32[:].rearrange("p (c g) -> p c g", g=GROUPS),
+            axis=mybir.AxisListType.X,
+            op=ALU.add,
+        )
+        group_ones = const.tile([P, PER_PIECE], BF16)
+        nc.vector.tensor_copy(out=group_ones[:], in_=group_ones_f32[:])
+        tiny = const.tile([P, 1], F32)
+        nc.vector.memset(tiny[:], TINY)
+
+        w_codes = [const.tile([P, N_OUT], U32, name="w_codes%d" % br, align_bytes=64) for br in BRANCHES]
+        w_scales = [const.tile([P, N_OUT], U8, name="w_scales%d" % br, align_bytes=64) for br in BRANCHES]
+        x_codes = [const.tile([P, ROWS], U32, name="x_codes%d" % br, align_bytes=64) for br in BRANCHES]
+        x_scales = [const.tile([P, ROWS], U8, name="x_scales%d" % br, align_bytes=64) for br in BRANCHES]
+
+        loaded_rf = {}
+        loaded_bb = {}
+
+        def load_rows(dram_rows):
+            rows = rf_loads.tile([P, SLABS, K], BF16)
+            nc.sync.dma_start(out=rows[:], in_=dram_rows.rearrange("(s p) k -> p s k", p=P))
+            return rows
+
+        def load_rf(blk):
+            loaded_rf[blk] = load_rows(RF_feature[blk * BLOCK : (blk + 1) * BLOCK, :])
+
+        def load_bb(blk):
+            wide = bb_loads.tile([P, GROUPS, K], BF16)
+            nc.sync.dma_start(out=wide[:], in_=BB_feature[blk * BLOCK + TENSOR_SLABS * P : (blk + 1) * BLOCK, :, :])
+            pair01 = sums.tile([P, K], F32)
+            nc.gpsimd.tensor_tensor(out=pair01[:], in0=wide[:, 0, :], in1=wide[:, 1, :], op=ALU.add)
+            pair23 = sums.tile([P, K], F32, bufs=2)
+            nc.gpsimd.tensor_tensor(out=pair23[:], in0=wide[:, 2, :], in1=wide[:, 3, :], op=ALU.add)
+            nc.gpsimd.tensor_tensor(out=pair01[:], in0=pair01[:], in1=pair23[:], op=ALU.add)
+            stacked_slabs = []
+            for s in range(TENSOR_SLABS):
+                stacked = bb_loads.tile([P, PIECES, K], BF16, bufs=(AHEAD + 1) * TENSOR_SLABS)
+                row0 = (blk * BLOCK + s * P) * GROUPS
+                nc.sync.dma_start(
+                    out=stacked[:], in_=bb_rows[row0 : row0 + P * GROUPS, :].rearrange("(i p) k -> p i k", p=P)
+                )
+                stacked_slabs.append(stacked)
+            loaded_bb[blk] = (stacked_slabs, pair01)
+
+        def regroup_by_words(rows):
+            words = rows[:].bitcast(F32)
+            grouped = regroup.tile([P, BLOCK, PACK], BF16, align_bytes=64)
+            grouped_words = grouped[:].bitcast(F32)
+            for half in range(SLABS // 2):
+                bank = front.tile([P, 2, 2, P], F32, tag="front")
+                for s in range(2):
+                    for u in range(2):
+                        nc.tensor.transpose(bank[:, s, u, :], words[:, 2 * half + s, u : K // 2 : 2], ident_f32[:])
+                nc.vector.tensor_copy(
+                    out=grouped_words[:, 2 * half * P : 2 * (half + 1) * P, :].rearrange("p (s r) u -> p s r u", s=2),
+                    in_=bank[:].rearrange("p s u r -> p s r u"),
+                )
+            return grouped
+
+        def regroup_mean_slab(grouped, stacked_slabs, last_slab_sum, s):
+            bank = front.tile([P, PACK, P], F32, tag="front")
+            if s < TENSOR_SLABS:
+                for i in range(PIECES):
+                    for t in range(PACK):
+                        nc.tensor.matmul(
+                            bank[:, t, i * PER_PIECE : (i + 1) * PER_PIECE],
+                            lhsT=stacked_slabs[s][:, i, t:K:PACK],
+                            rhs=group_ones[:],
+                            start=True,
+                            stop=True,
+                        )
+            else:
+                for t in range(PACK):
+                    nc.tensor.transpose(bank[:, t, :], last_slab_sum[:, t:K:PACK], ident_f32[:])
+            nc.vector.tensor_scalar(
+                out=grouped[:, s * P : (s + 1) * P, :],
+                in0=bank[:].rearrange("p t r -> p r t"),
+                scalar1=1.0 / GROUPS,
+                scalar2=None,
+                op0=ALU.mult,
+            )
+
+        def quantise(grouped, codes, scales):
+            nc.vector.quantize_mx(
+                out=codes.bitcast(FP8X4), scales=scales, in_=grouped[:].rearrange("p c t -> p (c t)")
+            )
+
+        def prepare_rf(blk):
+            cols = slice(blk * BLOCK, (blk + 1) * BLOCK)
+            quantise(regroup_by_words(loaded_rf[blk]), x_codes[RF][:, cols], x_scales[RF][:, cols])
+
+        grouped_means = {}
+
+        def prepare_bb_slab(blk, s):
+            if s == 0:
+                grouped = regroup.tile([P, BLOCK, PACK], BF16, align_bytes=64)
+                grouped_means[blk] = grouped
+            regroup_mean_slab(grouped_means[blk], *loaded_bb[blk], s)
+            if s == SLABS - 1:
+                cols = slice(blk * BLOCK, (blk + 1) * BLOCK)
+                quantise(grouped_means[blk], x_codes[BB][:, cols], x_scales[BB][:, cols])
+                if blk + AHEAD < BLOCKS:
+                    load_rf(blk + AHEAD)
+                    load_bb(blk + AHEAD)
+
+        def product(blk, chunk, br):
+            acc = products.tile([P, BLOCK], F32)
+            n_cols = slice(chunk * P, (chunk + 1) * P)
+            b_cols = slice(blk * BLOCK, (blk + 1) * BLOCK)
+            nc.tensor.matmul_mx(
+                out=acc[:],
+                lhsT=w_codes[br][:, n_cols].bitcast(FP8X4),
+                lhsT_scale=w_scales[br][:, n_cols],
+                rhs=x_codes[br][:, b_cols].bitcast(FP8X4),
+                rhs_scale=x_scales[br][:, b_cols],
+                start=True,
+                stop=True,
+            )
+            return acc
+
+        staged = {}
+
+        def sigmoid_step(blk, chunk, br):
+            if br == RF:
+                both = stage.tile([P, 2, BLOCK], F32)
+                staged[(blk, chunk)] = both
+            acc = product(blk, chunk, br)
+            col = br * CHUNKS + chunk
+            nc.scalar.activation(
+                out=staged[(blk, chunk)][:, br, :], in_=acc[:], func=ACT.Sigmoid, bias=bias_neg[:, col : col + 1], scale=-1.0
+            )
+
+        def log_step(blk, chunk):
+            flat = staged[(blk, chunk)][:].rearrange("p a b -> p (a b)")
+            nc.scalar.activation(out=flat, in_=flat, func=ACT.Ln, bias=tiny[:, 0:1], scale=1.0)
+
+        def tanh_step(blk, chunk):
+            flat = staged[(blk, chunk)][:].rearrange("p a b -> p (a b)")
+            nc.scalar.activation(out=flat, in_=flat, func=ACT.Tanh, scale=-1.0)
+
+        def mish_step(blk, chunk, br):
+            half = staged[(blk, chunk)][:, br, :]
+            acc = product(blk, chunk, br)
+            col = br * CHUNKS + chunk
+            nc.vector.scalar_tensor_tensor(
+                out=half, in0=acc[:], scalar=bias_pos[:, col : col + 1], in1=half, op0=ALU.add, op1=ALU.mult
+            )
+
+        def add_branches(blk, chunk):
+            both = staged[(blk, chunk)]
+            nc.gpsimd.tensor_tensor(out=both[:, RF, :], in0=both[:, RF, :], in1=both[:, BB, :], op=ALU.add)
+
+        def transpose_back(blk, chunk, on_scalar):
+            bank = back.tile([P, SLABS, P], F32)
+            for s in range(SLABS):
+                nc.tensor.transpose(bank[:, s, :], staged[(blk, chunk)][:, RF, s * P : (s + 1) * P], ident_f32[:])
+            piece = result.tile([P, SLABS, P], F32)
+            if on_scalar:
+                nc.scalar.copy(out=piece[:], in_=bank[:])
+            else:
+                nc.vector.tensor_copy(out=piece[:], in_=bank[:])
+            nc.sync.dma_start(
+                out=out[blk * BLOCK : (blk + 1) * BLOCK, chunk * P : (chunk + 1) * P].rearrange("(s p) n -> p s n", p=P),
+                in_=piece[:],
+            )
+
+        bias_rows = const.tile([P, P], BF16)
+        nc.vector.memset(bias_rows[:], 0.0)
+        nc.sync.dma_start(out=bias_rows[0:CHUNKS, :], in_=b_rfrf.rearrange("(c p) -> c p", p=P))
+        nc.sync.dma_start(out=bias_rows[CHUNKS : 2 * CHUNKS, :], in_=b_bbrf.rearrange("(c p) -> c p", p=P))
+        w_rf_rows = load_rows(W_rfrf)
+        load_rf(0)
+        w_bb_rows = load_rows(W_bbrf)
+        load_bb(0)
+        for blk in range(1, AHEAD):
+            load_rf(blk)
+            load_bb(blk)
+        bias_bank = front.tile([P, P], BF16, tag="front")
+        nc.tensor.transpose(bias_bank[:], bias_rows[:], ident_bf16[:])
+        bias_pos = const.tile([P, 2 * CHUNKS], F32)
+        nc.vector.tensor_copy(out=bias_pos[:], in_=bias_bank[:, 0 : 2 * CHUNKS])
+        bias_neg = const.tile([P, 2 * CHUNKS], F32)
+        nc.vector.tensor_scalar(
+            out=bias_neg[:], in0=bias_bank[:, 0 : 2 * CHUNKS], scalar1=-1.0, scalar2=None, op0=ALU.mult
+        )
+
+        quantise(regroup_by_words(w_rf_rows), w_codes[RF][:], w_scales[RF][:])
+        prepare_rf(0)
+        for chunk in range(CHUNKS):
+            sigmoid_step(0, chunk, RF)
+        quantise(regroup_by_words(w_bb_rows), w_codes[BB][:], w_scales[BB][:])
+        for blk in range(BATCH + 1):
+            if blk + 1 < BATCH:
+                prepare_rf(blk + 1)
+            for chunk in range(CHUNKS):
+                if blk < BATCH:
+                    prepare_bb_slab(blk, chunk)
+                if blk + 1 < BATCH:
+                    sigmoid_step(blk + 1, chunk, RF)
+                if blk > 0:
+                    sigmoid_step(blk - 1, chunk, BB)
+
+        all_steps = [(blk, chunk) for blk in range(BLOCKS) for chunk in range(CHUNKS)]
+
+        def trail(i, scalar_helps):
+            if 0 <= i - LAG < len(all_steps):
+                for br in BRANCHES:
+                    mish_step(*all_steps[i - LAG], br)
+                add_branches(*all_steps[i - LAG])
+            if 0 <= i - LAG - BEHIND < len(all_steps):
+                transpose_back(*all_steps[i - LAG - BEHIND], on_scalar=scalar_helps and i % 2 == 1)
+
+        for batch in range(BATCHES):
+            more = batch + 1 < BATCHES
+            steps = range(batch * STEPS, (batch + 1) * STEPS)
+            for i in steps:
+                log_step(*all_steps[i])
+            if more:
+                for blk in range((batch + 1) * BATCH, (batch + 2) * BATCH):
+                    prepare_rf(blk)
+                    for s in range(SLABS):
+                        prepare_bb_slab(blk, s)
+            if more:
+                for br in BRANCHES:
+                    sigmoid_step(*all_steps[steps[0] + STEPS], br)
+            for i in steps:
+                tanh_step(*all_steps[i])
+                if more and i < steps[-1]:
+                    for br in BRANCHES:
+                        sigmoid_step(*all_steps[i + 1 + STEPS], br)
+                trail(i, scalar_helps=not more)
+        for i in range(len(all_steps), len(all_steps) + LAG + BEHIND):
+            trail(i, scalar_helps=True)

@@ -19,10 +19,10 @@ BLOCK = 512
 BLOCKS = ROWS // BLOCK
 SLABS = BLOCK // P
 CHUNKS = N_OUT // P
-BATCH = 2
-BATCHES = BLOCKS // BATCH
-STEPS = BATCH * CHUNKS
-LAG = 1
+PAIR = 2
+PAIRS = CHUNKS // PAIR
+PREPARED = 4
+LAG = 2
 BEHIND = 2
 AHEAD = 2
 RF = 0
@@ -33,6 +33,13 @@ PIECES = P // PER_PIECE
 TENSOR_SLABS = 3
 TINY = 1e-18
 
+BATCHES = (
+    ((RF, 0), (RF, 1), (RF, 2), (RF, 3), (BB, 0),),
+    ((BB, 1), (BB, 2), (RF, 4), (BB, 3),),
+    ((RF, 5), (BB, 4), (RF, 6), (BB, 5),),
+    ((BB, 6), (RF, 7), (BB, 7),),
+)
+
 FLOPS = 2 * 2 * ROWS * K * N_OUT
 
 
@@ -41,20 +48,21 @@ def tile_gnn_layer_pa_t_kernel(tc, BB_feature, RF_feature, W_rfrf, b_rfrf, W_bbr
     bb_rows = BB_feature.rearrange("b g k -> (b g) k")
 
     with tc.manual_schedule(), tc.tile_pool(name="const", bufs=1) as const, tc.tile_pool(
-        name="rf_loads", bufs=AHEAD + 3
-    ) as rf_loads, tc.tile_pool(name="bb_loads", bufs=AHEAD + 1) as bb_loads, tc.tile_pool(
-        name="sums", bufs=AHEAD + 2
+        name="loads", bufs=15
+    ) as loads, tc.tile_pool(
+        name="sums", bufs=2
     ) as sums, tc.tile_pool(name="regroup", bufs=2) as regroup, tc.tile_pool(
-        name="stage", bufs=2 * STEPS
+        name="stage", bufs=22
     ) as stage, tc.tile_pool(
-        name="result", bufs=4
-    ) as result, tc.psum_pool(name="front", bufs=2) as front, tc.psum_pool(
-        name="products", bufs=4
-    ) as products, tc.psum_pool(name="back", bufs=2) as back:
+        name="result", bufs=2
+    ) as result, tc.psum_pool(name="work", bufs=6) as work, tc.psum_pool(name="back", bufs=2) as back:
+        warm = const.tile([P, 1], F32)
+        nc.vector.memset(warm[:], 0.0)
+        nc.scalar.activation(out=warm[:], in_=warm[:], func=ACT.Sigmoid)
         ident_f32 = const.tile([P, P], F32)
         make_identity(nc, ident_f32[:])
         ident_bf16 = const.tile([P, P], BF16)
-        make_identity(nc, ident_bf16[:])
+        nc.vector.tensor_copy(out=ident_bf16[:], in_=ident_f32[:])
         group_ones_f32 = const.tile([P, PER_PIECE], F32)
         nc.vector.tensor_reduce(
             out=group_ones_f32[:],
@@ -76,7 +84,7 @@ def tile_gnn_layer_pa_t_kernel(tc, BB_feature, RF_feature, W_rfrf, b_rfrf, W_bbr
         loaded_bb = {}
 
         def load_rows(dram_rows):
-            rows = rf_loads.tile([P, SLABS, K], BF16)
+            rows = loads.tile([P, SLABS, K], BF16, tag="loads")
             nc.sync.dma_start(out=rows[:], in_=dram_rows.rearrange("(s p) k -> p s k", p=P))
             return rows
 
@@ -84,40 +92,52 @@ def tile_gnn_layer_pa_t_kernel(tc, BB_feature, RF_feature, W_rfrf, b_rfrf, W_bbr
             loaded_rf[blk] = load_rows(RF_feature[blk * BLOCK : (blk + 1) * BLOCK, :])
 
         def load_bb(blk):
-            wide = bb_loads.tile([P, GROUPS, K], BF16)
+            wide = loads.tile([P, GROUPS, K], BF16, tag="loads")
             nc.sync.dma_start(out=wide[:], in_=BB_feature[blk * BLOCK + TENSOR_SLABS * P : (blk + 1) * BLOCK, :, :])
-            pair01 = sums.tile([P, K], F32)
-            nc.gpsimd.tensor_tensor(out=pair01[:], in0=wide[:, 0, :], in1=wide[:, 1, :], op=ALU.add)
-            pair23 = sums.tile([P, K], F32, bufs=2)
-            nc.gpsimd.tensor_tensor(out=pair23[:], in0=wide[:, 2, :], in1=wide[:, 3, :], op=ALU.add)
-            nc.gpsimd.tensor_tensor(out=pair01[:], in0=pair01[:], in1=pair23[:], op=ALU.add)
             stacked_slabs = []
             for s in range(TENSOR_SLABS):
-                stacked = bb_loads.tile([P, PIECES, K], BF16, bufs=(AHEAD + 1) * TENSOR_SLABS)
+                stacked = loads.tile([P, PIECES, K], BF16, tag="loads")
                 row0 = (blk * BLOCK + s * P) * GROUPS
                 nc.sync.dma_start(
                     out=stacked[:], in_=bb_rows[row0 : row0 + P * GROUPS, :].rearrange("(i p) k -> p i k", p=P)
                 )
                 stacked_slabs.append(stacked)
-            loaded_bb[blk] = (stacked_slabs, pair01)
+            loaded_bb[blk] = (stacked_slabs, wide)
 
-        def regroup_by_words(rows):
+        def add_last_slab(blk):
+            stacked_slabs, wide = loaded_bb[blk]
+            halves = []
+            for h in range(2):
+                half = sums.tile([P, K], F32, name="half%d" % h)
+                nc.gpsimd.tensor_tensor(out=half[:], in0=wide[:, 2 * h, :], in1=wide[:, 2 * h + 1, :], op=ALU.add)
+                halves.append(half)
+            loaded_bb[blk] = (stacked_slabs, halves)
+
+        def accumulate_transposes(dst, sources):
+            for n, src in enumerate(sources):
+                nc.tensor.matmul(
+                    dst, lhsT=src, rhs=ident_f32[:], start=n == 0, stop=n == len(sources) - 1, is_transpose=True
+                )
+
+        def regroup_by_words(rows, on_scalar=False):
             words = rows[:].bitcast(F32)
-            grouped = regroup.tile([P, BLOCK, PACK], BF16, align_bytes=64)
+            grouped = regroup.tile([P, BLOCK, PACK], BF16, tag="grouped", align_bytes=64)
             grouped_words = grouped[:].bitcast(F32)
             for half in range(SLABS // 2):
-                bank = front.tile([P, 2, 2, P], F32, tag="front")
+                bank = work.tile([P, 2, 2, P], F32, tag="work")
                 for s in range(2):
                     for u in range(2):
                         nc.tensor.transpose(bank[:, s, u, :], words[:, 2 * half + s, u : K // 2 : 2], ident_f32[:])
-                nc.vector.tensor_copy(
-                    out=grouped_words[:, 2 * half * P : 2 * (half + 1) * P, :].rearrange("p (s r) u -> p s r u", s=2),
-                    in_=bank[:].rearrange("p s u r -> p s r u"),
-                )
+                dst = grouped_words[:, 2 * half * P : 2 * (half + 1) * P, :].rearrange("p (s r) u -> p s r u", s=2)
+                src = bank[:].rearrange("p s u r -> p s r u")
+                if on_scalar:
+                    nc.scalar.copy(out=dst, in_=src)
+                else:
+                    nc.vector.tensor_copy(out=dst, in_=src)
             return grouped
 
-        def regroup_mean_slab(grouped, stacked_slabs, last_slab_sum, s):
-            bank = front.tile([P, PACK, P], F32, tag="front")
+        def regroup_mean_slab(grouped, stacked_slabs, halves, s):
+            bank = work.tile([P, PACK, P], F32, tag="work")
             if s < TENSOR_SLABS:
                 for i in range(PIECES):
                     for t in range(PACK):
@@ -130,7 +150,7 @@ def tile_gnn_layer_pa_t_kernel(tc, BB_feature, RF_feature, W_rfrf, b_rfrf, W_bbr
                         )
             else:
                 for t in range(PACK):
-                    nc.tensor.transpose(bank[:, t, :], last_slab_sum[:, t:K:PACK], ident_f32[:])
+                    accumulate_transposes(bank[:, t, :], [half[:, t:K:PACK] for half in halves])
             nc.vector.tensor_scalar(
                 out=grouped[:, s * P : (s + 1) * P, :],
                 in0=bank[:].rearrange("p t r -> p r t"),
@@ -144,26 +164,23 @@ def tile_gnn_layer_pa_t_kernel(tc, BB_feature, RF_feature, W_rfrf, b_rfrf, W_bbr
                 out=codes.bitcast(FP8X4), scales=scales, in_=grouped[:].rearrange("p c t -> p (c t)")
             )
 
-        def prepare_rf(blk):
+        def prepare(br, blk, on_scalar=False):
             cols = slice(blk * BLOCK, (blk + 1) * BLOCK)
-            quantise(regroup_by_words(loaded_rf[blk]), x_codes[RF][:, cols], x_scales[RF][:, cols])
+            if br == RF:
+                grouped = regroup_by_words(loaded_rf[blk], on_scalar)
+            else:
+                add_last_slab(blk)
+                grouped = regroup.tile([P, BLOCK, PACK], BF16, tag="grouped", align_bytes=64)
+                for s in range(SLABS):
+                    regroup_mean_slab(grouped, *loaded_bb[blk], s)
+            quantise(grouped, x_codes[br][:, cols], x_scales[br][:, cols])
+            if br == BB and blk + AHEAD < BLOCKS:
+                load_bb(blk + AHEAD)
+                if 1 <= blk <= 3:
+                    load_rf(blk + 4)
 
-        grouped_means = {}
-
-        def prepare_bb_slab(blk, s):
-            if s == 0:
-                grouped = regroup.tile([P, BLOCK, PACK], BF16, align_bytes=64)
-                grouped_means[blk] = grouped
-            regroup_mean_slab(grouped_means[blk], *loaded_bb[blk], s)
-            if s == SLABS - 1:
-                cols = slice(blk * BLOCK, (blk + 1) * BLOCK)
-                quantise(grouped_means[blk], x_codes[BB][:, cols], x_scales[BB][:, cols])
-                if blk + AHEAD < BLOCKS:
-                    load_rf(blk + AHEAD)
-                    load_bb(blk + AHEAD)
-
-        def product(blk, chunk, br):
-            acc = products.tile([P, BLOCK], F32)
+        def product(br, blk, chunk):
+            acc = work.tile([P, BLOCK], F32, tag="work")
             n_cols = slice(chunk * P, (chunk + 1) * P)
             b_cols = slice(blk * BLOCK, (blk + 1) * BLOCK)
             nc.tensor.matmul_mx(
@@ -179,62 +196,71 @@ def tile_gnn_layer_pa_t_kernel(tc, BB_feature, RF_feature, W_rfrf, b_rfrf, W_bbr
 
         staged = {}
 
-        def sigmoid_step(blk, chunk, br):
-            if br == RF:
-                both = stage.tile([P, 2, BLOCK], F32)
-                staged[(blk, chunk)] = both
-            acc = product(blk, chunk, br)
-            col = br * CHUNKS + chunk
-            nc.scalar.activation(
-                out=staged[(blk, chunk)][:, br, :], in_=acc[:], func=ACT.Sigmoid, bias=bias_neg[:, col : col + 1], scale=-1.0
-            )
+        def sigmoid_tile(br, blk, pair):
+            tile = stage.tile([P, PAIR, BLOCK], F32)
+            staged[(br, blk, pair)] = tile
+            for c in range(PAIR):
+                acc = product(br, blk, pair * PAIR + c)
+                col = br * CHUNKS + pair * PAIR + c
+                nc.scalar.activation(
+                    out=tile[:, c, :], in_=acc[:], func=ACT.Sigmoid, bias=bias_neg[:, col : col + 1], scale=-1.0
+                )
 
-        def log_step(blk, chunk):
-            flat = staged[(blk, chunk)][:].rearrange("p a b -> p (a b)")
+        def log_tile(br, blk, pair):
+            flat = staged[(br, blk, pair)][:].rearrange("p a b -> p (a b)")
             nc.scalar.activation(out=flat, in_=flat, func=ACT.Ln, bias=tiny[:, 0:1], scale=1.0)
 
-        def tanh_step(blk, chunk):
-            flat = staged[(blk, chunk)][:].rearrange("p a b -> p (a b)")
+        def tanh_tile(br, blk, pair):
+            flat = staged[(br, blk, pair)][:].rearrange("p a b -> p (a b)")
             nc.scalar.activation(out=flat, in_=flat, func=ACT.Tanh, scale=-1.0)
 
-        def mish_step(blk, chunk, br):
-            half = staged[(blk, chunk)][:, br, :]
-            acc = product(blk, chunk, br)
-            col = br * CHUNKS + chunk
-            nc.vector.scalar_tensor_tensor(
-                out=half, in0=acc[:], scalar=bias_pos[:, col : col + 1], in1=half, op0=ALU.add, op1=ALU.mult
-            )
+        def mish_tile(br, blk, pair):
+            tile = staged[(br, blk, pair)]
+            for c in range(PAIR):
+                acc = product(br, blk, pair * PAIR + c)
+                col = br * CHUNKS + pair * PAIR + c
+                nc.vector.scalar_tensor_tensor(
+                    out=tile[:, c, :],
+                    in0=acc[:],
+                    scalar=bias_pos[:, col : col + 1],
+                    in1=tile[:, c, :],
+                    op0=ALU.add,
+                    op1=ALU.mult,
+                )
 
-        def add_branches(blk, chunk):
-            both = staged[(blk, chunk)]
-            nc.gpsimd.tensor_tensor(out=both[:, RF, :], in0=both[:, RF, :], in1=both[:, BB, :], op=ALU.add)
-
-        def transpose_back(blk, chunk, on_scalar):
-            bank = back.tile([P, SLABS, P], F32)
-            for s in range(SLABS):
-                nc.tensor.transpose(bank[:, s, :], staged[(blk, chunk)][:, RF, s * P : (s + 1) * P], ident_f32[:])
-            piece = result.tile([P, SLABS, P], F32)
-            if on_scalar:
-                nc.scalar.copy(out=piece[:], in_=bank[:])
-            else:
-                nc.vector.tensor_copy(out=piece[:], in_=bank[:])
+        def way_back(blk, pair, scalar_helps):
+            piece = result.tile([P, SLABS, PAIR, P], F32)
+            for c in range(PAIR):
+                bank = back.tile([P, SLABS, P], F32, tag="back")
+                for s in range(SLABS):
+                    accumulate_transposes(
+                        bank[:, s, :], [staged[(br, blk, pair)][:, c, s * P : (s + 1) * P] for br in BRANCHES]
+                    )
+                if scalar_helps and c == 1:
+                    nc.scalar.copy(out=piece[:, :, c, :], in_=bank[:])
+                else:
+                    nc.vector.tensor_copy(out=piece[:, :, c, :], in_=bank[:])
+            n0 = pair * PAIR * P
             nc.sync.dma_start(
-                out=out[blk * BLOCK : (blk + 1) * BLOCK, chunk * P : (chunk + 1) * P].rearrange("(s p) n -> p s n", p=P),
-                in_=piece[:],
+                out=out[blk * BLOCK : (blk + 1) * BLOCK, n0 : n0 + PAIR * P].rearrange("(s p) n -> p s n", p=P),
+                in_=piece[:].rearrange("p s c n -> p s (c n)"),
             )
 
         bias_rows = const.tile([P, P], BF16)
         nc.vector.memset(bias_rows[:], 0.0)
-        nc.sync.dma_start(out=bias_rows[0:CHUNKS, :], in_=b_rfrf.rearrange("(c p) -> c p", p=P))
-        nc.sync.dma_start(out=bias_rows[CHUNKS : 2 * CHUNKS, :], in_=b_bbrf.rearrange("(c p) -> c p", p=P))
         w_rf_rows = load_rows(W_rfrf)
         load_rf(0)
+        nc.sync.dma_start(out=bias_rows[0:CHUNKS, :], in_=b_rfrf.rearrange("(c p) -> c p", p=P))
+        nc.sync.dma_start(out=bias_rows[CHUNKS : 2 * CHUNKS, :], in_=b_bbrf.rearrange("(c p) -> c p", p=P))
+        load_rf(1)
         w_bb_rows = load_rows(W_bbrf)
-        load_bb(0)
-        for blk in range(1, AHEAD):
+        quantise(regroup_by_words(w_rf_rows, on_scalar=True), w_codes[RF][:], w_scales[RF][:])
+        for blk in range(2, 5):
             load_rf(blk)
+        for blk in range(AHEAD):
             load_bb(blk)
-        bias_bank = front.tile([P, P], BF16, tag="front")
+        prepare(RF, 0)
+        bias_bank = work.tile([P, P], BF16, tag="work")
         nc.tensor.transpose(bias_bank[:], bias_rows[:], ident_bf16[:])
         bias_pos = const.tile([P, 2 * CHUNKS], F32)
         nc.vector.tensor_copy(out=bias_pos[:], in_=bias_bank[:, 0 : 2 * CHUNKS])
@@ -243,50 +269,59 @@ def tile_gnn_layer_pa_t_kernel(tc, BB_feature, RF_feature, W_rfrf, b_rfrf, W_bbr
             out=bias_neg[:], in0=bias_bank[:, 0 : 2 * CHUNKS], scalar1=-1.0, scalar2=None, op0=ALU.mult
         )
 
-        quantise(regroup_by_words(w_rf_rows), w_codes[RF][:], w_scales[RF][:])
-        prepare_rf(0)
-        for chunk in range(CHUNKS):
-            sigmoid_step(0, chunk, RF)
-        quantise(regroup_by_words(w_bb_rows), w_codes[BB][:], w_scales[BB][:])
-        for blk in range(BATCH + 1):
-            if blk + 1 < BATCH:
-                prepare_rf(blk + 1)
-            for chunk in range(CHUNKS):
-                if blk < BATCH:
-                    prepare_bb_slab(blk, chunk)
-                if blk + 1 < BATCH:
-                    sigmoid_step(blk + 1, chunk, RF)
-                if blk > 0:
-                    sigmoid_step(blk - 1, chunk, BB)
+        first = BATCHES[0]
+        for n, (br, blk) in enumerate(first):
+            if n + 1 < len(first):
+                if n == 1:
+                    quantise(regroup_by_words(w_bb_rows, on_scalar=True), w_codes[BB][:], w_scales[BB][:])
+                prepare(*first[n + 1])
+            for pair in range(PAIRS):
+                sigmoid_tile(br, blk, pair)
 
-        all_steps = [(blk, chunk) for blk in range(BLOCKS) for chunk in range(CHUNKS)]
+        def tiles_of(batch):
+            return sorted(((br, blk, pair) for br, blk in batch for pair in range(PAIRS)), key=lambda x: (x[1], x[2], x[0]))
 
-        def trail(i, scalar_helps):
-            if 0 <= i - LAG < len(all_steps):
-                for br in BRANCHES:
-                    mish_step(*all_steps[i - LAG], br)
-                add_branches(*all_steps[i - LAG])
-            if 0 <= i - LAG - BEHIND < len(all_steps):
-                transpose_back(*all_steps[i - LAG - BEHIND], on_scalar=scalar_helps and i % 2 == 1)
+        multiplied = []
+        returned = set()
 
-        for batch in range(BATCHES):
-            more = batch + 1 < BATCHES
-            steps = range(batch * STEPS, (batch + 1) * STEPS)
-            for i in steps:
-                log_step(*all_steps[i])
-            if more:
-                for blk in range((batch + 1) * BATCH, (batch + 2) * BATCH):
-                    prepare_rf(blk)
-                    for s in range(SLABS):
-                        prepare_bb_slab(blk, s)
-            if more:
-                for br in BRANCHES:
-                    sigmoid_step(*all_steps[steps[0] + STEPS], br)
-            for i in steps:
-                tanh_step(*all_steps[i])
-                if more and i < steps[-1]:
-                    for br in BRANCHES:
-                        sigmoid_step(*all_steps[i + 1 + STEPS], br)
-                trail(i, scalar_helps=not more)
-        for i in range(len(all_steps), len(all_steps) + LAG + BEHIND):
-            trail(i, scalar_helps=True)
+        def multiply(tile, scalar_helps=False):
+            if tile is not None:
+                mish_tile(*tile)
+            multiplied.append(tile)
+            if len(multiplied) > BEHIND and multiplied[-1 - BEHIND] is not None:
+                br, blk, pair = multiplied[-1 - BEHIND]
+                ready = multiplied[: len(multiplied) - BEHIND]
+                if (blk, pair) not in returned and all((b, blk, pair) in ready for b in BRANCHES):
+                    returned.add((blk, pair))
+                    way_back(blk, pair, scalar_helps)
+
+        waiting = []
+        for b, batch in enumerate(BATCHES):
+            last = b + 1 == len(BATCHES)
+            tiles = tiles_of(batch)
+            following = () if last else BATCHES[b + 1]
+            sigmoids = [(br, blk, pair) for br, blk in following for pair in range(PAIRS)]
+            for tile in tiles:
+                log_tile(*tile)
+            prepared = 0
+            while prepared < min(PREPARED, len(following)):
+                prepare(*following[prepared])
+                prepared += 1
+            woven = 0
+            for n, tile in enumerate(tiles):
+                while woven < len(sigmoids) and woven * len(tiles) <= n * len(sigmoids):
+                    sigmoid_tile(*sigmoids[woven])
+                    woven += 1
+                    if woven % PAIRS == 0 and prepared < len(following):
+                        prepare(*following[prepared])
+                        prepared += 1
+                tanh_tile(*tile)
+                waiting.append(tile)
+                if len(waiting) > LAG:
+                    multiply(waiting.pop(0), scalar_helps=last)
+            for tile in sigmoids[woven:]:
+                sigmoid_tile(*tile)
+        while waiting:
+            multiply(waiting.pop(0), scalar_helps=True)
+        for n in range(BEHIND):
+            multiply(None, scalar_helps=True)

@@ -22,15 +22,24 @@ CHUNKS = N_OUT // P
 PAIR = 2
 PAIRS = CHUNKS // PAIR
 PREPARED = 4
+TAIL_LAG = 1
 LAG = 2
 BEHIND = 2
+SUMS = 4
+LOADS = 14
+PIECES_PER_BEAT = 1
+EXTRA_LN = 0
+DIVIDE_AFTER = 11
+MULTIPLY_AFTER = 8
+DIV_TILES = 4
+STAGES = 18
 AHEAD = 2
 RF = 0
 BB = 1
 BRANCHES = (RF, BB)
 PER_PIECE = P // GROUPS
 PIECES = P // PER_PIECE
-TENSOR_SLABS = 3
+TENSOR_SLABS = (3, 3, 3, 3, 3, 3, 3, 4)
 TINY = 1e-18
 
 BATCHES = (
@@ -40,6 +49,8 @@ BATCHES = (
     ((BB, 6), (RF, 7), (BB, 7),),
 )
 
+DIVIDED = ((0,1), (1,1), )
+
 FLOPS = 2 * 2 * ROWS * K * N_OUT
 
 
@@ -48,11 +59,11 @@ def tile_gnn_layer_pa_t_kernel(tc, BB_feature, RF_feature, W_rfrf, b_rfrf, W_bbr
     bb_rows = BB_feature.rearrange("b g k -> (b g) k")
 
     with tc.manual_schedule(), tc.tile_pool(name="const", bufs=1) as const, tc.tile_pool(
-        name="loads", bufs=15
+        name="loads", bufs=LOADS
     ) as loads, tc.tile_pool(
-        name="sums", bufs=2
-    ) as sums, tc.tile_pool(name="regroup", bufs=2) as regroup, tc.tile_pool(
-        name="stage", bufs=22
+        name="sums", bufs=SUMS
+    ) as sums, tc.tile_pool(name="regroup", bufs=2) as regroup, tc.tile_pool(name="quotient", bufs=1) as quotient, tc.tile_pool(
+        name="stage", bufs=STAGES
     ) as stage, tc.tile_pool(
         name="result", bufs=2
     ) as result, tc.psum_pool(name="work", bufs=6) as work, tc.psum_pool(name="back", bufs=2) as back:
@@ -83,35 +94,57 @@ def tile_gnn_layer_pa_t_kernel(tc, BB_feature, RF_feature, W_rfrf, b_rfrf, W_bbr
         loaded_rf = {}
         loaded_bb = {}
 
-        def load_rows(dram_rows):
+        def load_rows(dram_rows, pieces=1):
             rows = loads.tile([P, SLABS, K], BF16, tag="loads")
-            nc.sync.dma_start(out=rows[:], in_=dram_rows.rearrange("(s p) k -> p s k", p=P))
+            src = dram_rows.rearrange("(s p) k -> p s k", p=P)
+            step = SLABS // pieces
+            for s in range(0, SLABS, step):
+                nc.sync.dma_start(out=rows[:, s : s + step, :], in_=src[:, s : s + step, :])
             return rows
 
-        def load_rf(blk):
-            loaded_rf[blk] = load_rows(RF_feature[blk * BLOCK : (blk + 1) * BLOCK, :])
+        def load_rf(blk, pieces=1):
+            loaded_rf[blk] = load_rows(RF_feature[blk * BLOCK : (blk + 1) * BLOCK, :], pieces)
+
+        means = {}
+
+        def add_on_gpsimd(blk):
+            for s in range(TENSOR_SLABS[blk], SLABS):
+                rows = loaded_bb[blk][s]
+                halves = []
+                for h in range(2):
+                    half = sums.tile([P, K], F32, name="half%d" % h)
+                    nc.gpsimd.tensor_tensor(out=half[:], in0=rows[:, 2 * h, :], in1=rows[:, 2 * h + 1, :], op=ALU.add)
+                    halves.append(half)
+                means[(blk, s)] = halves
 
         def load_bb(blk):
-            wide = loads.tile([P, GROUPS, K], BF16, tag="loads")
-            nc.sync.dma_start(out=wide[:], in_=BB_feature[blk * BLOCK + TENSOR_SLABS * P : (blk + 1) * BLOCK, :, :])
-            stacked_slabs = []
-            for s in range(TENSOR_SLABS):
-                stacked = loads.tile([P, PIECES, K], BF16, tag="loads")
-                row0 = (blk * BLOCK + s * P) * GROUPS
-                nc.sync.dma_start(
-                    out=stacked[:], in_=bb_rows[row0 : row0 + P * GROUPS, :].rearrange("(i p) k -> p i k", p=P)
-                )
-                stacked_slabs.append(stacked)
-            loaded_bb[blk] = (stacked_slabs, wide)
+            slabs = [None] * SLABS
+            for s in reversed(range(SLABS)):
+                row0 = blk * BLOCK + s * P
+                rows = loads.tile([P, GROUPS, K], BF16, tag="loads")
+                if s < TENSOR_SLABS[blk]:
+                    src = bb_rows[row0 * GROUPS : (row0 + P) * GROUPS, :].rearrange("(i p) k -> p i k", p=P)
+                else:
+                    src = BB_feature[row0 : row0 + P, :, :]
+                nc.sync.dma_start(out=rows[:], in_=src)
+                slabs[s] = rows
+            loaded_bb[blk] = slabs
 
-        def add_last_slab(blk):
-            stacked_slabs, wide = loaded_bb[blk]
-            halves = []
-            for h in range(2):
-                half = sums.tile([P, K], F32, name="half%d" % h)
-                nc.gpsimd.tensor_tensor(out=half[:], in0=wide[:, 2 * h, :], in1=wide[:, 2 * h + 1, :], op=ALU.add)
-                halves.append(half)
-            loaded_bb[blk] = (stacked_slabs, halves)
+        to_load = [unit for batch in BATCHES for unit in batch]
+        held = [0]
+
+        def tiles_for(br):
+            return SLABS if br == BB else 1
+
+        def top_up():
+            while to_load and held[0] + tiles_for(to_load[0][0]) <= LOADS:
+                br, blk = to_load.pop(0)
+                held[0] += tiles_for(br)
+                (load_bb if br == BB else load_rf)(blk)
+
+        def consumed(br):
+            held[0] -= tiles_for(br)
+            top_up()
 
         def accumulate_transposes(dst, sources):
             for n, src in enumerate(sources):
@@ -119,38 +152,38 @@ def tile_gnn_layer_pa_t_kernel(tc, BB_feature, RF_feature, W_rfrf, b_rfrf, W_bbr
                     dst, lhsT=src, rhs=ident_f32[:], start=n == 0, stop=n == len(sources) - 1, is_transpose=True
                 )
 
-        def regroup_by_words(rows, on_scalar=False):
-            words = rows[:].bitcast(F32)
-            grouped = regroup.tile([P, BLOCK, PACK], BF16, tag="grouped", align_bytes=64)
-            grouped_words = grouped[:].bitcast(F32)
-            for half in range(SLABS // 2):
-                bank = work.tile([P, 2, 2, P], F32, tag="work")
-                for s in range(2):
-                    for u in range(2):
-                        nc.tensor.transpose(bank[:, s, u, :], words[:, 2 * half + s, u : K // 2 : 2], ident_f32[:])
-                dst = grouped_words[:, 2 * half * P : 2 * (half + 1) * P, :].rearrange("p (s r) u -> p s r u", s=2)
-                src = bank[:].rearrange("p s u r -> p s r u")
-                if on_scalar:
-                    nc.scalar.copy(out=dst, in_=src)
-                else:
-                    nc.vector.tensor_copy(out=dst, in_=src)
-            return grouped
+        def new_grouped():
+            return regroup.tile([P, BLOCK, PACK], BF16, name="grouped", align_bytes=64)
 
-        def regroup_mean_slab(grouped, stacked_slabs, halves, s):
+        def regroup_words(grouped, rows, half, on_scalar=False):
+            words = rows[:].bitcast(F32)
+            bank = work.tile([P, 2, 2, P], F32, tag="work")
+            for s in range(2):
+                for u in range(2):
+                    nc.tensor.transpose(bank[:, s, u, :], words[:, 2 * half + s, u : K // 2 : 2], ident_f32[:])
+            grouped_words = grouped[:].bitcast(F32)
+            dst = grouped_words[:, 2 * half * P : 2 * (half + 1) * P, :].rearrange("p (s r) u -> p s r u", s=2)
+            src = bank[:].rearrange("p s u r -> p s r u")
+            if on_scalar:
+                nc.scalar.copy(out=dst, in_=src)
+            else:
+                nc.vector.tensor_copy(out=dst, in_=src)
+
+        def regroup_mean_slab(grouped, blk, s):
             bank = work.tile([P, PACK, P], F32, tag="work")
-            if s < TENSOR_SLABS:
+            if s < TENSOR_SLABS[blk]:
                 for i in range(PIECES):
                     for t in range(PACK):
                         nc.tensor.matmul(
                             bank[:, t, i * PER_PIECE : (i + 1) * PER_PIECE],
-                            lhsT=stacked_slabs[s][:, i, t:K:PACK],
+                            lhsT=loaded_bb[blk][s][:, i, t:K:PACK],
                             rhs=group_ones[:],
                             start=True,
                             stop=True,
                         )
             else:
                 for t in range(PACK):
-                    accumulate_transposes(bank[:, t, :], [half[:, t:K:PACK] for half in halves])
+                    accumulate_transposes(bank[:, t, :], [half[:, t:K:PACK] for half in means[(blk, s)]])
             nc.vector.tensor_scalar(
                 out=grouped[:, s * P : (s + 1) * P, :],
                 in0=bank[:].rearrange("p t r -> p r t"),
@@ -164,20 +197,57 @@ def tile_gnn_layer_pa_t_kernel(tc, BB_feature, RF_feature, W_rfrf, b_rfrf, W_bbr
                 out=codes.bitcast(FP8X4), scales=scales, in_=grouped[:].rearrange("p c t -> p (c t)")
             )
 
-        def prepare(br, blk, on_scalar=False):
-            cols = slice(blk * BLOCK, (blk + 1) * BLOCK)
+        pieces = []
+
+        def queue_unit(br, blk):
+            box = []
+
+            def words(half):
+                if half == 0:
+                    box.append(new_grouped())
+                regroup_words(box[0], loaded_rf[blk], half)
+
+            def mean(s):
+                if s == 0:
+                    box.append(new_grouped())
+                    add_loaded(blk)
+                regroup_mean_slab(box[0], blk, s)
+
+            def finish():
+                cols = slice(blk * BLOCK, (blk + 1) * BLOCK)
+                quantise(box[0], x_codes[br][:, cols], x_scales[br][:, cols])
+                consumed(br)
+
             if br == RF:
-                grouped = regroup_by_words(loaded_rf[blk], on_scalar)
+                for half in range(SLABS // 2):
+                    pieces.append(((br, blk), words, half))
             else:
-                add_last_slab(blk)
-                grouped = regroup.tile([P, BLOCK, PACK], BF16, tag="grouped", align_bytes=64)
                 for s in range(SLABS):
-                    regroup_mean_slab(grouped, *loaded_bb[blk], s)
-            quantise(grouped, x_codes[br][:, cols], x_scales[br][:, cols])
-            if br == BB and blk + AHEAD < BLOCKS:
-                load_bb(blk + AHEAD)
-                if 1 <= blk <= 3:
-                    load_rf(blk + 4)
+                    pieces.append(((br, blk), mean, s))
+            pieces.append(((br, blk), finish, None))
+
+        added = set()
+
+        def add_loaded(upto=BLOCKS):
+            for blk in sorted(loaded_bb):
+                if blk not in added and blk <= upto:
+                    added.add(blk)
+                    add_on_gpsimd(blk)
+
+        def run_piece():
+            unit, do, arg = pieces.pop(0)
+            if arg is None:
+                do()
+            else:
+                do(arg)
+
+        def ensure(unit):
+            while any(p[0] == unit for p in pieces):
+                run_piece()
+
+        def prepare(br, blk):
+            queue_unit(br, blk)
+            ensure((br, blk))
 
         def product(br, blk, chunk):
             acc = work.tile([P, BLOCK], F32, tag="work")
@@ -197,7 +267,10 @@ def tile_gnn_layer_pa_t_kernel(tc, BB_feature, RF_feature, W_rfrf, b_rfrf, W_bbr
         staged = {}
 
         def sigmoid_tile(br, blk, pair):
-            tile = stage.tile([P, PAIR, BLOCK], F32)
+            if (blk, pair) in DIVIDED:
+                tile = quotient.tile([P, PAIR, BLOCK], F32, tag="divided", bufs=DIV_TILES)
+            else:
+                tile = stage.tile([P, PAIR, BLOCK], F32, tag="stage")
             staged[(br, blk, pair)] = tile
             for c in range(PAIR):
                 acc = product(br, blk, pair * PAIR + c)
@@ -213,6 +286,44 @@ def tile_gnn_layer_pa_t_kernel(tc, BB_feature, RF_feature, W_rfrf, b_rfrf, W_bbr
         def tanh_tile(br, blk, pair):
             flat = staged[(br, blk, pair)][:].rearrange("p a b -> p (a b)")
             nc.scalar.activation(out=flat, in_=flat, func=ACT.Tanh, scale=-1.0)
+
+        quotients = {}
+
+        def divide_before(blk, pair):
+            both = [staged[(br, blk, pair)] for br in BRANCHES]
+            for tile in both:
+                for c in range(PAIR):
+                    nc.gpsimd.tensor_tensor(out=tile[:, c, :], in0=tile[:, c, :], in1=tile[:, c, :], op=ALU.mult)
+                for c in range(PAIR):
+                    nc.gpsimd.tensor_scalar(
+                        out=tile[:, c, :], in0=tile[:, c, :], scalar1=1.0, scalar2=1.0, op0=ALU.mult, op1=ALU.add
+                    )
+            twos = quotient.tile([P, PAIR, BLOCK], F32)
+            for c in range(PAIR):
+                nc.gpsimd.tensor_tensor(out=twos[:, c, :], in0=both[RF][:, c, :], in1=both[BB][:, c, :], op=ALU.mult)
+            four = quotient.tile([P, BLOCK], F32)
+            nc.gpsimd.tensor_tensor(out=four[:], in0=twos[:, 0, :], in1=twos[:, 1, :], op=ALU.mult)
+            quotients[(blk, pair)] = (twos, four)
+
+        def divide(blk, pair, part):
+            twos, four = quotients[(blk, pair)]
+            nc.vector.reciprocal(out=four[:, part], in_=four[:, part])
+
+        def divide_after(blk, pair):
+            twos, inverse = quotients[(blk, pair)]
+            halves = quotient.tile([P, PAIR, BLOCK], F32, bufs=1)
+            for c in range(PAIR):
+                nc.gpsimd.tensor_tensor(out=halves[:, c, :], in0=inverse[:], in1=twos[:, 1 - c, :], op=ALU.mult)
+            both = [staged[(br, blk, pair)] for br in BRANCHES]
+            for c in range(PAIR):
+                nc.gpsimd.tensor_tensor(out=twos[:, c, :], in0=halves[:, c, :], in1=both[BB][:, c, :], op=ALU.mult)
+                nc.gpsimd.tensor_tensor(out=both[BB][:, c, :], in0=halves[:, c, :], in1=both[RF][:, c, :], op=ALU.mult)
+                nc.gpsimd.tensor_scalar(
+                    out=both[RF][:, c, :], in0=twos[:, c, :], scalar1=2.0, scalar2=-1.0, op0=ALU.mult, op1=ALU.add
+                )
+                nc.gpsimd.tensor_scalar(
+                    out=both[BB][:, c, :], in0=both[BB][:, c, :], scalar1=2.0, scalar2=-1.0, op0=ALU.mult, op1=ALU.add
+                )
 
         def mish_tile(br, blk, pair):
             tile = staged[(br, blk, pair)]
@@ -248,32 +359,44 @@ def tile_gnn_layer_pa_t_kernel(tc, BB_feature, RF_feature, W_rfrf, b_rfrf, W_bbr
 
         bias_rows = const.tile([P, P], BF16)
         nc.vector.memset(bias_rows[:], 0.0)
-        w_rf_rows = load_rows(W_rfrf)
-        load_rf(0)
-        nc.sync.dma_start(out=bias_rows[0:CHUNKS, :], in_=b_rfrf.rearrange("(c p) -> c p", p=P))
-        nc.sync.dma_start(out=bias_rows[CHUNKS : 2 * CHUNKS, :], in_=b_bbrf.rearrange("(c p) -> c p", p=P))
+        w_rf_rows = load_rows(W_rfrf, pieces=2)
+        to_load.remove((RF, 0))
+        load_rf(0, pieces=2)
+        nc.scalar.dma_start(out=bias_rows[0:CHUNKS, :], in_=b_rfrf.rearrange("(c p) -> c p", p=P))
+        nc.scalar.dma_start(out=bias_rows[CHUNKS : 2 * CHUNKS, :], in_=b_bbrf.rearrange("(c p) -> c p", p=P))
+        to_load.remove((RF, 1))
         load_rf(1)
         w_bb_rows = load_rows(W_bbrf)
-        quantise(regroup_by_words(w_rf_rows, on_scalar=True), w_codes[RF][:], w_scales[RF][:])
-        for blk in range(2, 5):
-            load_rf(blk)
-        for blk in range(AHEAD):
-            load_bb(blk)
-        prepare(RF, 0)
+        held[0] = 4
+        top_up()
+        w_rf_grouped = new_grouped()
+        for half in range(2):
+            regroup_words(w_rf_grouped, w_rf_rows, half, on_scalar=True)
+        consumed(RF)
+        grouped = new_grouped()
+        for half in range(2):
+            regroup_words(grouped, loaded_rf[0], half)
+        consumed(RF)
         bias_bank = work.tile([P, P], BF16, tag="work")
         nc.tensor.transpose(bias_bank[:], bias_rows[:], ident_bf16[:])
         bias_pos = const.tile([P, 2 * CHUNKS], F32)
-        nc.vector.tensor_copy(out=bias_pos[:], in_=bias_bank[:, 0 : 2 * CHUNKS])
         bias_neg = const.tile([P, 2 * CHUNKS], F32)
+        quantise(w_rf_grouped, w_codes[RF][:], w_scales[RF][:])
         nc.vector.tensor_scalar(
             out=bias_neg[:], in0=bias_bank[:, 0 : 2 * CHUNKS], scalar1=-1.0, scalar2=None, op0=ALU.mult
         )
+        quantise(grouped, x_codes[RF][:, 0:BLOCK], x_scales[RF][:, 0:BLOCK])
+        nc.vector.tensor_copy(out=bias_pos[:], in_=bias_bank[:, 0 : 2 * CHUNKS])
 
         first = BATCHES[0]
         for n, (br, blk) in enumerate(first):
             if n + 1 < len(first):
                 if n == 1:
-                    quantise(regroup_by_words(w_bb_rows, on_scalar=True), w_codes[BB][:], w_scales[BB][:])
+                    grouped = new_grouped()
+                    for half in range(2):
+                        regroup_words(grouped, w_bb_rows, half, on_scalar=True)
+                    quantise(grouped, w_codes[BB][:], w_scales[BB][:])
+                    consumed(RF)
                 prepare(*first[n + 1])
             for pair in range(PAIRS):
                 sigmoid_tile(br, blk, pair)
@@ -295,33 +418,71 @@ def tile_gnn_layer_pa_t_kernel(tc, BB_feature, RF_feature, W_rfrf, b_rfrf, W_bbr
                     returned.add((blk, pair))
                     way_back(blk, pair, scalar_helps)
 
+        beats = []
+        later = []
+
+        def beat():
+            beats.append(0)
+            for n in range(PIECES_PER_BEAT):
+                if pieces:
+                    run_piece()
+            for entry in list(later):
+                if entry[0] <= len(beats):
+                    later.remove(entry)
+                    entry[1](*entry[2])
+
+        def start_division(blk, pair):
+            divide_before(blk, pair)
+            now = len(beats)
+            for n in range(4):
+                later.append((now + DIVIDE_AFTER + n, divide, (blk, pair, slice(n * P, (n + 1) * P))))
+            later.append((now + DIVIDE_AFTER + 4, finish_division, (blk, pair)))
+
+        def finish_division(blk, pair):
+            add_loaded()
+            divide_after(blk, pair)
+            now = len(beats)
+            for br in BRANCHES:
+                later.append((now + MULTIPLY_AFTER + 2 * br, multiply, ((br, blk, pair),)))
+
         waiting = []
         for b, batch in enumerate(BATCHES):
             last = b + 1 == len(BATCHES)
-            tiles = tiles_of(batch)
+            tiles = [t for t in tiles_of(batch) if (t[1], t[2]) not in DIVIDED]
             following = () if last else BATCHES[b + 1]
             sigmoids = [(br, blk, pair) for br, blk in following for pair in range(PAIRS)]
-            for tile in tiles:
+            add_loaded()
+            for unit in following:
+                queue_unit(*unit)
+            for n, tile in enumerate(tiles):
                 log_tile(*tile)
-            prepared = 0
-            while prepared < min(PREPARED, len(following)):
-                prepare(*following[prepared])
-                prepared += 1
+                beat()
+                for k in range(EXTRA_LN):
+                    if pieces:
+                        run_piece()
+                if waiting and n >= 1:
+                    multiply(waiting.pop(0))
+            if b < len(DIVIDED):
+                start_division(*DIVIDED[b])
             woven = 0
             for n, tile in enumerate(tiles):
                 while woven < len(sigmoids) and woven * len(tiles) <= n * len(sigmoids):
+                    ensure(sigmoids[woven][:2])
                     sigmoid_tile(*sigmoids[woven])
                     woven += 1
-                    if woven % PAIRS == 0 and prepared < len(following):
-                        prepare(*following[prepared])
-                        prepared += 1
+                    beat()
                 tanh_tile(*tile)
                 waiting.append(tile)
-                if len(waiting) > LAG:
-                    multiply(waiting.pop(0), scalar_helps=last)
+                while len(waiting) > (TAIL_LAG if last else LAG):
+                    multiply(waiting.pop(0), scalar_helps=last and n % 2 == 1)
+                beat()
             for tile in sigmoids[woven:]:
+                ensure(tile[:2])
                 sigmoid_tile(*tile)
+                beat()
         while waiting:
             multiply(waiting.pop(0), scalar_helps=True)
+        while later:
+            beat()
         for n in range(BEHIND):
             multiply(None, scalar_helps=True)

@@ -23,19 +23,21 @@ PAIR = 2
 PAIRS = CHUNKS // PAIR
 PREPARED = 4
 TAIL_LAG = 1
+TAIL_HELP = 9
 LAG = 2
 BEHIND = 2
-SUMS = 4
-LOADS = 14
-PIECES_PER_BEAT = 1
+SUMS = 3
+LOADS = 13
+WBB_S = 0
+PIECES_PER_BEAT = 2
 EXTRA_LN = 0
 DIVIDE_AFTER = 11
 MULTIPLY_AFTER = 8
-DIV_TILES = 4
-STAGES = 18
+STAGES = 24
 AHEAD = 2
 RF = 0
 BB = 1
+WEIGHTS = 2
 BRANCHES = (RF, BB)
 PER_PIECE = P // GROUPS
 PIECES = P // PER_PIECE
@@ -49,7 +51,7 @@ BATCHES = (
     ((BB, 6), (RF, 7), (BB, 7),),
 )
 
-DIVIDED = ((0,1), (1,1), )
+DIVIDED = {(0,1): (0,0), (3,1): (1,0)}
 
 FLOPS = 2 * 2 * ROWS * K * N_OUT
 
@@ -131,6 +133,7 @@ def tile_gnn_layer_pa_t_kernel(tc, BB_feature, RF_feature, W_rfrf, b_rfrf, W_bbr
             loaded_bb[blk] = slabs
 
         to_load = [unit for batch in BATCHES for unit in batch]
+        to_load.insert(to_load.index((BB, 0)), (WEIGHTS, 0))
         held = [0]
 
         def tiles_for(br):
@@ -140,7 +143,12 @@ def tile_gnn_layer_pa_t_kernel(tc, BB_feature, RF_feature, W_rfrf, b_rfrf, W_bbr
             while to_load and held[0] + tiles_for(to_load[0][0]) <= LOADS:
                 br, blk = to_load.pop(0)
                 held[0] += tiles_for(br)
-                (load_bb if br == BB else load_rf)(blk)
+                if br == BB:
+                    load_bb(blk)
+                elif br == RF:
+                    load_rf(blk)
+                else:
+                    loaded_rf["weights"] = load_rows(W_bbrf)
 
         def consumed(br):
             held[0] -= tiles_for(br)
@@ -267,10 +275,7 @@ def tile_gnn_layer_pa_t_kernel(tc, BB_feature, RF_feature, W_rfrf, b_rfrf, W_bbr
         staged = {}
 
         def sigmoid_tile(br, blk, pair):
-            if (blk, pair) in DIVIDED:
-                tile = quotient.tile([P, PAIR, BLOCK], F32, tag="divided", bufs=DIV_TILES)
-            else:
-                tile = stage.tile([P, PAIR, BLOCK], F32, tag="stage")
+            tile = stage.tile([P, PAIR, BLOCK], F32, tag="stage")
             staged[(br, blk, pair)] = tile
             for c in range(PAIR):
                 acc = product(br, blk, pair * PAIR + c)
@@ -362,39 +367,38 @@ def tile_gnn_layer_pa_t_kernel(tc, BB_feature, RF_feature, W_rfrf, b_rfrf, W_bbr
         w_rf_rows = load_rows(W_rfrf, pieces=2)
         to_load.remove((RF, 0))
         load_rf(0, pieces=2)
-        nc.scalar.dma_start(out=bias_rows[0:CHUNKS, :], in_=b_rfrf.rearrange("(c p) -> c p", p=P))
-        nc.scalar.dma_start(out=bias_rows[CHUNKS : 2 * CHUNKS, :], in_=b_bbrf.rearrange("(c p) -> c p", p=P))
+        nc.sync.dma_start(out=bias_rows[0:CHUNKS, :], in_=b_rfrf.rearrange("(c p) -> c p", p=P))
+        nc.sync.dma_start(out=bias_rows[CHUNKS : 2 * CHUNKS, :], in_=b_bbrf.rearrange("(c p) -> c p", p=P))
         to_load.remove((RF, 1))
         load_rf(1)
-        w_bb_rows = load_rows(W_bbrf)
-        held[0] = 4
+        held[0] = 3
         top_up()
         w_rf_grouped = new_grouped()
         for half in range(2):
-            regroup_words(w_rf_grouped, w_rf_rows, half, on_scalar=True)
+            regroup_words(w_rf_grouped, w_rf_rows, half, on_scalar=half == 0)
         consumed(RF)
         grouped = new_grouped()
-        for half in range(2):
-            regroup_words(grouped, loaded_rf[0], half)
+        regroup_words(grouped, loaded_rf[0], 0, on_scalar=True)
+        quantise(w_rf_grouped, w_codes[RF][:], w_scales[RF][:])
+        regroup_words(grouped, loaded_rf[0], 1)
         consumed(RF)
+        quantise(grouped, x_codes[RF][:, 0:BLOCK], x_scales[RF][:, 0:BLOCK])
         bias_bank = work.tile([P, P], BF16, tag="work")
         nc.tensor.transpose(bias_bank[:], bias_rows[:], ident_bf16[:])
         bias_pos = const.tile([P, 2 * CHUNKS], F32)
         bias_neg = const.tile([P, 2 * CHUNKS], F32)
-        quantise(w_rf_grouped, w_codes[RF][:], w_scales[RF][:])
         nc.vector.tensor_scalar(
             out=bias_neg[:], in0=bias_bank[:, 0 : 2 * CHUNKS], scalar1=-1.0, scalar2=None, op0=ALU.mult
         )
-        quantise(grouped, x_codes[RF][:, 0:BLOCK], x_scales[RF][:, 0:BLOCK])
         nc.vector.tensor_copy(out=bias_pos[:], in_=bias_bank[:, 0 : 2 * CHUNKS])
 
         first = BATCHES[0]
         for n, (br, blk) in enumerate(first):
             if n + 1 < len(first):
-                if n == 1:
+                if first[n + 1] == (BB, 0):
                     grouped = new_grouped()
                     for half in range(2):
-                        regroup_words(grouped, w_bb_rows, half, on_scalar=True)
+                        regroup_words(grouped, loaded_rf["weights"], half, on_scalar=half < WBB_S)
                     quantise(grouped, w_codes[BB][:], w_scales[BB][:])
                     consumed(RF)
                 prepare(*first[n + 1])
@@ -462,8 +466,6 @@ def tile_gnn_layer_pa_t_kernel(tc, BB_feature, RF_feature, W_rfrf, b_rfrf, W_bbr
                         run_piece()
                 if waiting and n >= 1:
                     multiply(waiting.pop(0))
-            if b < len(DIVIDED):
-                start_division(*DIVIDED[b])
             woven = 0
             for n, tile in enumerate(tiles):
                 while woven < len(sigmoids) and woven * len(tiles) <= n * len(sigmoids):
@@ -471,10 +473,13 @@ def tile_gnn_layer_pa_t_kernel(tc, BB_feature, RF_feature, W_rfrf, b_rfrf, W_bbr
                     sigmoid_tile(*sigmoids[woven])
                     woven += 1
                     beat()
+                for q, place in DIVIDED.items():
+                    if place == (b, n):
+                        start_division(*q)
                 tanh_tile(*tile)
                 waiting.append(tile)
                 while len(waiting) > (TAIL_LAG if last else LAG):
-                    multiply(waiting.pop(0), scalar_helps=last and n % 2 == 1)
+                    multiply(waiting.pop(0), scalar_helps=last and n >= len(tiles) - TAIL_HELP)
                 beat()
             for tile in sigmoids[woven:]:
                 ensure(tile[:2])

@@ -24,10 +24,13 @@ PAIRS = CHUNKS // PAIR
 PREPARED = 4
 TAIL_LAG = 1
 TAIL_HELP = 9
+LN_HELPS = False
 LAG = 2
-BEHIND = 2
+BEHIND = 1
 SUMS = 3
-LOADS = 13
+LOADS = 12
+RESULTS = 3
+KEPT = (8, 8)
 WBB_S = 0
 PIECES_PER_BEAT = 2
 EXTRA_LN = 0
@@ -45,13 +48,13 @@ TENSOR_SLABS = (3, 3, 3, 3, 3, 3, 3, 4)
 TINY = 1e-18
 
 BATCHES = (
-    ((RF, 0), (RF, 1), (RF, 2), (RF, 3), (BB, 0),),
-    ((BB, 1), (BB, 2), (RF, 4), (BB, 3),),
-    ((RF, 5), (BB, 4), (RF, 6), (BB, 5),),
-    ((BB, 6), (RF, 7), (BB, 7),),
+    ((RF, 0), (RF, 1), (RF, 2), (RF, 3), (RF, 4), (BB, 0),),
+    ((BB, 1), (BB, 2), (BB, 3), (RF, 5), (RF, 6),),
+    ((BB, 4), (BB, 5), (RF, 7), (BB, 6),),
+    ((BB, 7),),
 )
 
-DIVIDED = {(0,1): (0,0), (3,1): (1,0)}
+DIVIDED = {(0,1): (0,1,0), (3,1): (1,1,0)}
 
 FLOPS = 2 * 2 * ROWS * K * N_OUT
 
@@ -64,10 +67,10 @@ def tile_gnn_layer_pa_t_kernel(tc, BB_feature, RF_feature, W_rfrf, b_rfrf, W_bbr
         name="loads", bufs=LOADS
     ) as loads, tc.tile_pool(
         name="sums", bufs=SUMS
-    ) as sums, tc.tile_pool(name="regroup", bufs=2) as regroup, tc.tile_pool(name="quotient", bufs=1) as quotient, tc.tile_pool(
+    ) as sums, tc.tile_pool(name="regroup", bufs=2) as regroup, tc.tile_pool(name="quotient", bufs=2) as quotient, tc.tile_pool(name="quantised", bufs=1) as quantised, tc.tile_pool(
         name="stage", bufs=STAGES
     ) as stage, tc.tile_pool(
-        name="result", bufs=2
+        name="result", bufs=RESULTS
     ) as result, tc.psum_pool(name="work", bufs=6) as work, tc.psum_pool(name="back", bufs=2) as back:
         warm = const.tile([P, 1], F32)
         nc.vector.memset(warm[:], 0.0)
@@ -90,8 +93,7 @@ def tile_gnn_layer_pa_t_kernel(tc, BB_feature, RF_feature, W_rfrf, b_rfrf, W_bbr
 
         w_codes = [const.tile([P, N_OUT], U32, name="w_codes%d" % br, align_bytes=64) for br in BRANCHES]
         w_scales = [const.tile([P, N_OUT], U8, name="w_scales%d" % br, align_bytes=64) for br in BRANCHES]
-        x_codes = [const.tile([P, ROWS], U32, name="x_codes%d" % br, align_bytes=64) for br in BRANCHES]
-        x_scales = [const.tile([P, ROWS], U8, name="x_scales%d" % br, align_bytes=64) for br in BRANCHES]
+        x_quantised = {}
 
         loaded_rf = {}
         loaded_bb = {}
@@ -205,6 +207,12 @@ def tile_gnn_layer_pa_t_kernel(tc, BB_feature, RF_feature, W_rfrf, b_rfrf, W_bbr
                 out=codes.bitcast(FP8X4), scales=scales, in_=grouped[:].rearrange("p c t -> p (c t)")
             )
 
+        def quantise_block(grouped, br, blk):
+            codes = quantised.tile([P, BLOCK], U32, name="x_codes%d" % br, bufs=KEPT[br], align_bytes=64)
+            scales = quantised.tile([P, BLOCK], U8, name="x_scales%d" % br, bufs=KEPT[br], align_bytes=64)
+            quantise(grouped, codes[:], scales[:])
+            x_quantised[(br, blk)] = (codes, scales)
+
         pieces = []
 
         def queue_unit(br, blk):
@@ -222,8 +230,7 @@ def tile_gnn_layer_pa_t_kernel(tc, BB_feature, RF_feature, W_rfrf, b_rfrf, W_bbr
                 regroup_mean_slab(box[0], blk, s)
 
             def finish():
-                cols = slice(blk * BLOCK, (blk + 1) * BLOCK)
-                quantise(box[0], x_codes[br][:, cols], x_scales[br][:, cols])
+                quantise_block(box[0], br, blk)
                 consumed(br)
 
             if br == RF:
@@ -260,13 +267,13 @@ def tile_gnn_layer_pa_t_kernel(tc, BB_feature, RF_feature, W_rfrf, b_rfrf, W_bbr
         def product(br, blk, chunk):
             acc = work.tile([P, BLOCK], F32, tag="work")
             n_cols = slice(chunk * P, (chunk + 1) * P)
-            b_cols = slice(blk * BLOCK, (blk + 1) * BLOCK)
+            codes, scales = x_quantised[(br, blk)]
             nc.tensor.matmul_mx(
                 out=acc[:],
                 lhsT=w_codes[br][:, n_cols].bitcast(FP8X4),
                 lhsT_scale=w_scales[br][:, n_cols],
-                rhs=x_codes[br][:, b_cols].bitcast(FP8X4),
-                rhs_scale=x_scales[br][:, b_cols],
+                rhs=codes[:].bitcast(FP8X4),
+                rhs_scale=scales[:],
                 start=True,
                 stop=True,
             )
@@ -288,9 +295,12 @@ def tile_gnn_layer_pa_t_kernel(tc, BB_feature, RF_feature, W_rfrf, b_rfrf, W_bbr
             flat = staged[(br, blk, pair)][:].rearrange("p a b -> p (a b)")
             nc.scalar.activation(out=flat, in_=flat, func=ACT.Ln, bias=tiny[:, 0:1], scale=1.0)
 
-        def tanh_tile(br, blk, pair):
+        def tanh_tile(br, blk, pair, pieces=1):
             flat = staged[(br, blk, pair)][:].rearrange("p a b -> p (a b)")
-            nc.scalar.activation(out=flat, in_=flat, func=ACT.Tanh, scale=-1.0)
+            step = PAIR * BLOCK // pieces
+            for c0 in range(0, PAIR * BLOCK, step):
+                part = flat[:, c0 : c0 + step]
+                nc.scalar.activation(out=part, in_=part, func=ACT.Tanh, scale=-1.0)
 
         quotients = {}
 
@@ -344,7 +354,7 @@ def tile_gnn_layer_pa_t_kernel(tc, BB_feature, RF_feature, W_rfrf, b_rfrf, W_bbr
                     op1=ALU.mult,
                 )
 
-        def way_back(blk, pair, scalar_helps):
+        def way_back(blk, pair, scalar_helps, chunkwise=False):
             piece = result.tile([P, SLABS, PAIR, P], F32)
             for c in range(PAIR):
                 bank = back.tile([P, SLABS, P], F32, tag="back")
@@ -356,11 +366,17 @@ def tile_gnn_layer_pa_t_kernel(tc, BB_feature, RF_feature, W_rfrf, b_rfrf, W_bbr
                     nc.scalar.copy(out=piece[:, :, c, :], in_=bank[:])
                 else:
                     nc.vector.tensor_copy(out=piece[:, :, c, :], in_=bank[:])
-            n0 = pair * PAIR * P
+                if chunkwise:
+                    store(blk, pair * PAIR + c, 1, piece[:, :, c, :])
+            if not chunkwise:
+                store(blk, pair * PAIR, PAIR, piece[:].rearrange("p s c n -> p s (c n)"))
+
+        def store(blk, chunk, chunks, src):
+            n0 = chunk * P
             nc.sync.dma_start(
-                out=out[blk * BLOCK : (blk + 1) * BLOCK, n0 : n0 + PAIR * P].rearrange("(s p) n -> p s n", p=P),
-                in_=piece[:].rearrange("p s c n -> p s (c n)"),
+                out=out[blk * BLOCK : (blk + 1) * BLOCK, n0 : n0 + chunks * P].rearrange("(s p) n -> p s n", p=P), in_=src
             )
+
 
         bias_rows = const.tile([P, P], BF16)
         nc.vector.memset(bias_rows[:], 0.0)
@@ -382,7 +398,7 @@ def tile_gnn_layer_pa_t_kernel(tc, BB_feature, RF_feature, W_rfrf, b_rfrf, W_bbr
         quantise(w_rf_grouped, w_codes[RF][:], w_scales[RF][:])
         regroup_words(grouped, loaded_rf[0], 1)
         consumed(RF)
-        quantise(grouped, x_codes[RF][:, 0:BLOCK], x_scales[RF][:, 0:BLOCK])
+        quantise_block(grouped, RF, 0)
         bias_bank = work.tile([P, P], BF16, tag="work")
         nc.tensor.transpose(bias_bank[:], bias_rows[:], ident_bf16[:])
         bias_pos = const.tile([P, 2 * CHUNKS], F32)
@@ -420,7 +436,7 @@ def tile_gnn_layer_pa_t_kernel(tc, BB_feature, RF_feature, W_rfrf, b_rfrf, W_bbr
                 ready = multiplied[: len(multiplied) - BEHIND]
                 if (blk, pair) not in returned and all((b, blk, pair) in ready for b in BRANCHES):
                     returned.add((blk, pair))
-                    way_back(blk, pair, scalar_helps)
+                    way_back(blk, pair, scalar_helps, chunkwise=(blk, pair) == (BLOCKS - 1, PAIRS - 1))
 
         beats = []
         later = []
@@ -442,6 +458,11 @@ def tile_gnn_layer_pa_t_kernel(tc, BB_feature, RF_feature, W_rfrf, b_rfrf, W_bbr
                 later.append((now + DIVIDE_AFTER + n, divide, (blk, pair, slice(n * P, (n + 1) * P))))
             later.append((now + DIVIDE_AFTER + 4, finish_division, (blk, pair)))
 
+        def start_divisions(*here):
+            for q, place in DIVIDED.items():
+                if place == here:
+                    start_division(*q)
+
         def finish_division(blk, pair):
             add_loaded()
             divide_after(blk, pair)
@@ -460,12 +481,13 @@ def tile_gnn_layer_pa_t_kernel(tc, BB_feature, RF_feature, W_rfrf, b_rfrf, W_bbr
                 queue_unit(*unit)
             for n, tile in enumerate(tiles):
                 log_tile(*tile)
+                start_divisions(b, 0, n)
                 beat()
                 for k in range(EXTRA_LN):
                     if pieces:
                         run_piece()
                 if waiting and n >= 1:
-                    multiply(waiting.pop(0))
+                    multiply(waiting.pop(0), scalar_helps=last and LN_HELPS)
             woven = 0
             for n, tile in enumerate(tiles):
                 while woven < len(sigmoids) and woven * len(tiles) <= n * len(sigmoids):
@@ -473,10 +495,8 @@ def tile_gnn_layer_pa_t_kernel(tc, BB_feature, RF_feature, W_rfrf, b_rfrf, W_bbr
                     sigmoid_tile(*sigmoids[woven])
                     woven += 1
                     beat()
-                for q, place in DIVIDED.items():
-                    if place == (b, n):
-                        start_division(*q)
-                tanh_tile(*tile)
+                start_divisions(b, 1, n)
+                tanh_tile(*tile, pieces=PAIR if last and n == len(tiles) - 1 else 1)
                 waiting.append(tile)
                 while len(waiting) > (TAIL_LAG if last else LAG):
                     multiply(waiting.pop(0), scalar_helps=last and n >= len(tiles) - TAIL_HELP)

@@ -32,7 +32,9 @@ LOADS = 12
 RESULTS = 3
 KEPT = (8, 8)
 WBB_S = 0
-PIECES_PER_BEAT = 2
+P_SIG = 1
+LOG_PIECES = (2, 2, 1)
+P_TANH = 1
 EXTRA_LN = 0
 DIVIDE_AFTER = 11
 MULTIPLY_AFTER = 8
@@ -441,9 +443,9 @@ def tile_gnn_layer_pa_t_kernel(tc, BB_feature, RF_feature, W_rfrf, b_rfrf, W_bbr
         beats = []
         later = []
 
-        def beat():
+        def beat(count):
             beats.append(0)
-            for n in range(PIECES_PER_BEAT):
+            for n in range(count):
                 if pieces:
                     run_piece()
             for entry in list(later):
@@ -482,7 +484,7 @@ def tile_gnn_layer_pa_t_kernel(tc, BB_feature, RF_feature, W_rfrf, b_rfrf, W_bbr
             for n, tile in enumerate(tiles):
                 log_tile(*tile)
                 start_divisions(b, 0, n)
-                beat()
+                beat(LOG_PIECES[n % len(LOG_PIECES)])
                 for k in range(EXTRA_LN):
                     if pieces:
                         run_piece()
@@ -494,20 +496,20 @@ def tile_gnn_layer_pa_t_kernel(tc, BB_feature, RF_feature, W_rfrf, b_rfrf, W_bbr
                     ensure(sigmoids[woven][:2])
                     sigmoid_tile(*sigmoids[woven])
                     woven += 1
-                    beat()
+                    beat(P_SIG)
                 start_divisions(b, 1, n)
                 tanh_tile(*tile, pieces=PAIR if last and n == len(tiles) - 1 else 1)
                 waiting.append(tile)
                 while len(waiting) > (TAIL_LAG if last else LAG):
                     multiply(waiting.pop(0), scalar_helps=last and n >= len(tiles) - TAIL_HELP)
-                beat()
+                beat(P_TANH)
             for tile in sigmoids[woven:]:
                 ensure(tile[:2])
                 sigmoid_tile(*tile)
-                beat()
+                beat(2)
         while waiting:
             multiply(waiting.pop(0), scalar_helps=True)
         while later:
-            beat()
+            beat(2)
         for n in range(BEHIND):
             multiply(None, scalar_helps=True)

import concourse.mybir as mybir
from concourse.masks import make_identity

F32 = mybir.dt.float32
BF16 = mybir.dt.bfloat16
U32 = mybir.dt.uint32
U8 = mybir.dt.uint8
FP8X4 = mybir.dt.float8_e4m3fn_x4
ACT = mybir.ActivationFunctionType
ALU = mybir.AluOpType

P = 128
PACK = 4
ROWS = 4096
GROUPS = 4
K = 512
N_OUT = 512
BLOCK = 512
BLOCKS = ROWS // BLOCK
SLABS = BLOCK // P
CHUNKS = N_OUT // P
PAIR = 2
PAIRS = CHUNKS // PAIR
PREPARED = 4
TAIL_LAG = 1
TAIL_HELP = 9
LN_HELPS = False
LAG = 2
BEHIND = 1
SUMS = 3
LOADS = 12
RESULTS = 3
KEPT = (8, 8)
WBB_S = 0
P_SIG = 1
LOG_PIECES = (2, 2, 1)
P_TANH = 1
EXTRA_LN = 0
DIVIDE_AFTER = 11
MULTIPLY_AFTER = 8
STAGES = 24
AHEAD = 2
RF = 0
BB = 1
WEIGHTS = 2
BRANCHES = (RF, BB)
PER_PIECE = P // GROUPS
PIECES = P // PER_PIECE
TENSOR_SLABS = (3, 3, 3, 3, 3, 3, 3, 4)
TINY = 1e-18

BATCHES = (
    ((RF, 0), (RF, 1), (RF, 2), (RF, 3), (RF, 4), (BB, 0),),
    ((BB, 1), (BB, 2), (BB, 3), (RF, 5), (RF, 6),),
    ((BB, 4), (BB, 5), (RF, 7), (BB, 6),),
    ((BB, 7),),
)

DIVIDED = {(0,1): (0,1,0), (3,1): (1,1,0)}

FLOPS = 2 * 2 * ROWS * K * N_OUT


def tile_gnn_layer_pa_t_kernel(tc, BB_feature, RF_feature, W_rfrf, b_rfrf, W_bbrf, b_bbrf, out):
    nc = tc.nc
    bb_rows = BB_feature.rearrange("b g k -> (b g) k")

    with tc.manual_schedule(), tc.tile_pool(name="const", bufs=1) as const, tc.tile_pool(
        name="loads", bufs=LOADS
    ) as loads, tc.tile_pool(
        name="sums", bufs=SUMS
    ) as sums, tc.tile_pool(name="regroup", bufs=2) as regroup, tc.tile_pool(name="quotient", bufs=2) as quotient, tc.tile_pool(name="quantised", bufs=1) as quantised, tc.tile_pool(
        name="stage", bufs=STAGES
    ) as stage, tc.tile_pool(
        name="result", bufs=RESULTS
    ) as result, tc.psum_pool(name="work", bufs=6) as work, tc.psum_pool(name="back", bufs=2) as back:
        warm = const.tile([P, 1], F32)
        nc.vector.memset(warm[:], 0.0)
        nc.scalar.activation(out=warm[:], in_=warm[:], func=ACT.Sigmoid)
        ident_f32 = const.tile([P, P], F32)
        make_identity(nc, ident_f32[:])
        ident_bf16 = const.tile([P, P], BF16)
        nc.vector.tensor_copy(out=ident_bf16[:], in_=ident_f32[:])
        group_ones_f32 = const.tile([P, PER_PIECE], F32)
        nc.vector.tensor_reduce(
            out=group_ones_f32[:],
            in_=ident_f32[:].rearrange("p (c g) -> p c g", g=GROUPS),
            axis=mybir.AxisListType.X,
            op=ALU.add,
        )
        group_ones = const.tile([P, PER_PIECE], BF16)
        nc.vector.tensor_copy(out=group_ones[:], in_=group_ones_f32[:])
        tiny = const.tile([P, 1], F32)
        nc.vector.memset(tiny[:], TINY)

        w_codes = [const.tile([P, N_OUT], U32, name="w_codes%d" % br, align_bytes=64) for br in BRANCHES]
        w_scales = [const.tile([P, N_OUT], U8, name="w_scales%d" % br, align_bytes=64) for br in BRANCHES]
        x_quantised = {}

        loaded_rf = {}
        loaded_bb = {}

        def load_rows(dram_rows, pieces=1):
            rows = loads.tile([P, SLABS, K], BF16, tag="loads")
            src = dram_rows.rearrange("(s p) k -> p s k", p=P)
            step = SLABS // pieces
            for s in range(0, SLABS, step):
                nc.sync.dma_start(out=rows[:, s : s + step, :], in_=src[:, s : s + step, :])
            return rows

        def load_rf(blk, pieces=1):
            loaded_rf[blk] = load_rows(RF_feature[blk * BLOCK : (blk + 1) * BLOCK, :], pieces)

        means = {}

        def add_on_gpsimd(blk):
            for s in range(TENSOR_SLABS[blk], SLABS):
                rows = loaded_bb[blk][s]
                halves = []
                for h in range(2):
                    half = sums.tile([P, K], F32, name="half%d" % h)
                    nc.gpsimd.tensor_tensor(out=half[:], in0=rows[:, 2 * h, :], in1=rows[:, 2 * h + 1, :], op=ALU.add)
                    halves.append(half)
                means[(blk, s)] = halves

        def load_bb(blk):
            slabs = [None] * SLABS
            for s in reversed(range(SLABS)):
                row0 = blk * BLOCK + s * P
                rows = loads.tile([P, GROUPS, K], BF16, tag="loads")
                if s < TENSOR_SLABS[blk]:
                    src = bb_rows[row0 * GROUPS : (row0 + P) * GROUPS, :].rearrange("(i p) k -> p i k", p=P)
                else:
                    src = BB_feature[row0 : row0 + P, :, :]
                nc.sync.dma_start(out=rows[:], in_=src)
                slabs[s] = rows
            loaded_bb[blk] = slabs

        to_load = [unit for batch in BATCHES for unit in batch]
        to_load.insert(to_load.index((BB, 0)), (WEIGHTS, 0))
        held = [0]

        def tiles_for(br):
            return SLABS if br == BB else 1

        def top_up():
            while to_load and held[0] + tiles_for(to_load[0][0]) <= LOADS:
                br, blk = to_load.pop(0)
                held[0] += tiles_for(br)
                if br == BB:
                    load_bb(blk)
                elif br == RF:
                    load_rf(blk)
                else:
                    loaded_rf["weights"] = load_rows(W_bbrf)

        def consumed(br):
            held[0] -= tiles_for(br)
            top_up()

        def accumulate_transposes(dst, sources):
            for n, src in enumerate(sources):
                nc.tensor.matmul(
                    dst, lhsT=src, rhs=ident_f32[:], start=n == 0, stop=n == len(sources) - 1, is_transpose=True
                )

        def new_grouped():
            return regroup.tile([P, BLOCK, PACK], BF16, name="grouped", align_bytes=64)

        def regroup_words(grouped, rows, half, on_scalar=False):
            words = rows[:].bitcast(F32)
            bank = work.tile([P, 2, 2, P], F32, tag="work")
            for s in range(2):
                for u in range(2):
                    nc.tensor.transpose(bank[:, s, u, :], words[:, 2 * half + s, u : K // 2 : 2], ident_f32[:])
            grouped_words = grouped[:].bitcast(F32)
            dst = grouped_words[:, 2 * half * P : 2 * (half + 1) * P, :].rearrange("p (s r) u -> p s r u", s=2)
            src = bank[:].rearrange("p s u r -> p s r u")
            if on_scalar:
                nc.scalar.copy(out=dst, in_=src)
            else:
                nc.vector.tensor_copy(out=dst, in_=src)

        def regroup_mean_slab(grouped, blk, s):
            bank = work.tile([P, PACK, P], F32, tag="work")
            if s < TENSOR_SLABS[blk]:
                for i in range(PIECES):
                    for t in range(PACK):
                        nc.tensor.matmul(
                            bank[:, t, i * PER_PIECE : (i + 1) * PER_PIECE],
                            lhsT=loaded_bb[blk][s][:, i, t:K:PACK],
                            rhs=group_ones[:],
                            start=True,
                            stop=True,
                        )
            else:
                for t in range(PACK):
                    accumulate_transposes(bank[:, t, :], [half[:, t:K:PACK] for half in means[(blk, s)]])
            nc.vector.tensor_scalar(
                out=grouped[:, s * P : (s + 1) * P, :],
                in0=bank[:].rearrange("p t r -> p r t"),
                scalar1=1.0 / GROUPS,
                scalar2=None,
                op0=ALU.mult,
            )

        def quantise(grouped, codes, scales):
            nc.vector.quantize_mx(
                out=codes.bitcast(FP8X4), scales=scales, in_=grouped[:].rearrange("p c t -> p (c t)")
            )

        def quantise_block(grouped, br, blk):
            codes = quantised.tile([P, BLOCK], U32, name="x_codes%d" % br, bufs=KEPT[br], align_bytes=64)
            scales = quantised.tile([P, BLOCK], U8, name="x_scales%d" % br, bufs=KEPT[br], align_bytes=64)
            quantise(grouped, codes[:], scales[:])
            x_quantised[(br, blk)] = (codes, scales)

        pieces = []

        def queue_unit(br, blk):
            box = []

            def words(half):
                if half == 0:
                    box.append(new_grouped())
                regroup_words(box[0], loaded_rf[blk], half)

            def mean(s):
                if s == 0:
                    box.append(new_grouped())
                    add_loaded(blk)
                regroup_mean_slab(box[0], blk, s)

            def finish():
                quantise_block(box[0], br, blk)
                consumed(br)

            if br == RF:
                for half in range(SLABS // 2):
                    pieces.append(((br, blk), words, half))
            else:
                for s in range(SLABS):
                    pieces.append(((br, blk), mean, s))
            pieces.append(((br, blk), finish, None))

        added = set()

        def add_loaded(upto=BLOCKS):
            for blk in sorted(loaded_bb):
                if blk not in added and blk <= upto:
                    added.add(blk)
                    add_on_gpsimd(blk)

        def run_piece():
            unit, do, arg = pieces.pop(0)
            if arg is None:
                do()
            else:
                do(arg)

        def ensure(unit):
            while any(p[0] == unit for p in pieces):
                run_piece()

        def prepare(br, blk):
            queue_unit(br, blk)
            ensure((br, blk))

        def product(br, blk, chunk):
            acc = work.tile([P, BLOCK], F32, tag="work")
            n_cols = slice(chunk * P, (chunk + 1) * P)
            codes, scales = x_quantised[(br, blk)]
            nc.tensor.matmul_mx(
                out=acc[:],
                lhsT=w_codes[br][:, n_cols].bitcast(FP8X4),
                lhsT_scale=w_scales[br][:, n_cols],
                rhs=codes[:].bitcast(FP8X4),
                rhs_scale=scales[:],
                start=True,
                stop=True,
            )
            return acc

        staged = {}

        def sigmoid_tile(br, blk, pair):
            tile = stage.tile([P, PAIR, BLOCK], F32, tag="stage")
            staged[(br, blk, pair)] = tile
            for c in range(PAIR):
                acc = product(br, blk, pair * PAIR + c)
                col = br * CHUNKS + pair * PAIR + c
                nc.scalar.activation(
                    out=tile[:, c, :], in_=acc[:], func=ACT.Sigmoid, bias=bias_neg[:, col : col + 1], scale=-1.0
                )

        def log_tile(br, blk, pair):
            flat = staged[(br, blk, pair)][:].rearrange("p a b -> p (a b)")
            nc.scalar.activation(out=flat, in_=flat, func=ACT.Ln, bias=tiny[:, 0:1], scale=1.0)

        def tanh_tile(br, blk, pair, pieces=1):
            flat = staged[(br, blk, pair)][:].rearrange("p a b -> p (a b)")
            step = PAIR * BLOCK // pieces
            for c0 in range(0, PAIR * BLOCK, step):
                part = flat[:, c0 : c0 + step]
                nc.scalar.activation(out=part, in_=part, func=ACT.Tanh, scale=-1.0)

        quotients = {}

        def divide_before(blk, pair):
            both = [staged[(br, blk, pair)] for br in BRANCHES]
            for tile in both:
                for c in range(PAIR):
                    nc.gpsimd.tensor_tensor(out=tile[:, c, :], in0=tile[:, c, :], in1=tile[:, c, :], op=ALU.mult)
                for c in range(PAIR):
                    nc.gpsimd.tensor_scalar(
                        out=tile[:, c, :], in0=tile[:, c, :], scalar1=1.0, scalar2=1.0, op0=ALU.mult, op1=ALU.add
                    )
            twos = quotient.tile([P, PAIR, BLOCK], F32)
            for c in range(PAIR):
                nc.gpsimd.tensor_tensor(out=twos[:, c, :], in0=both[RF][:, c, :], in1=both[BB][:, c, :], op=ALU.mult)
            four = quotient.tile([P, BLOCK], F32)
            nc.gpsimd.tensor_tensor(out=four[:], in0=twos[:, 0, :], in1=twos[:, 1, :], op=ALU.mult)
            quotients[(blk, pair)] = (twos, four)

        def divide(blk, pair, part):
            twos, four = quotients[(blk, pair)]
            nc.vector.reciprocal(out=four[:, part], in_=four[:, part])

        def divide_after(blk, pair):
            twos, inverse = quotients[(blk, pair)]
            halves = quotient.tile([P, PAIR, BLOCK], F32, bufs=1)
            for c in range(PAIR):
                nc.gpsimd.tensor_tensor(out=halves[:, c, :], in0=inverse[:], in1=twos[:, 1 - c, :], op=ALU.mult)
            both = [staged[(br, blk, pair)] for br in BRANCHES]
            for c in range(PAIR):
                nc.gpsimd.tensor_tensor(out=twos[:, c, :], in0=halves[:, c, :], in1=both[BB][:, c, :], op=ALU.mult)
                nc.gpsimd.tensor_tensor(out=both[BB][:, c, :], in0=halves[:, c, :], in1=both[RF][:, c, :], op=ALU.mult)
                nc.gpsimd.tensor_scalar(
                    out=both[RF][:, c, :], in0=twos[:, c, :], scalar1=2.0, scalar2=-1.0, op0=ALU.mult, op1=ALU.add
                )
                nc.gpsimd.tensor_scalar(
                    out=both[BB][:, c, :], in0=both[BB][:, c, :], scalar1=2.0, scalar2=-1.0, op0=ALU.mult, op1=ALU.add
                )

        def mish_tile(br, blk, pair):
            tile = staged[(br, blk, pair)]
            for c in range(PAIR):
                acc = product(br, blk, pair * PAIR + c)
                col = br * CHUNKS + pair * PAIR + c
                nc.vector.scalar_tensor_tensor(
                    out=tile[:, c, :],
                    in0=acc[:],
                    scalar=bias_pos[:, col : col + 1],
                    in1=tile[:, c, :],
                    op0=ALU.add,
                    op1=ALU.mult,
                )

        def way_back(blk, pair, scalar_helps, chunkwise=False):
            piece = result.tile([P, SLABS, PAIR, P], F32)
            for c in range(PAIR):
                bank = back.tile([P, SLABS, P], F32, tag="back")
                for s in range(SLABS):
                    accumulate_transposes(
                        bank[:, s, :], [staged[(br, blk, pair)][:, c, s * P : (s + 1) * P] for br in BRANCHES]
                    )
                if scalar_helps and c == 1:
                    nc.scalar.copy(out=piece[:, :, c, :], in_=bank[:])
                else:
                    nc.vector.tensor_copy(out=piece[:, :, c, :], in_=bank[:])
                if chunkwise:
                    store(blk, pair * PAIR + c, 1, piece[:, :, c, :])
            if not chunkwise:
                store(blk, pair * PAIR, PAIR, piece[:].rearrange("p s c n -> p s (c n)"))

        def store(blk, chunk, chunks, src):
            n0 = chunk * P
            nc.sync.dma_start(
                out=out[blk * BLOCK : (blk + 1) * BLOCK, n0 : n0 + chunks * P].rearrange("(s p) n -> p s n", p=P), in_=src
            )


        bias_rows = const.tile([P, P], BF16)
        nc.vector.memset(bias_rows[:], 0.0)
        w_rf_rows = load_rows(W_rfrf, pieces=2)
        to_load.remove((RF, 0))
        load_rf(0, pieces=2)
        nc.sync.dma_start(out=bias_rows[0:CHUNKS, :], in_=b_rfrf.rearrange("(c p) -> c p", p=P))
        nc.sync.dma_start(out=bias_rows[CHUNKS : 2 * CHUNKS, :], in_=b_bbrf.rearrange("(c p) -> c p", p=P))
        to_load.remove((RF, 1))
        load_rf(1)
        held[0] = 3
        top_up()
        w_rf_grouped = new_grouped()
        for half in range(2):
            regroup_words(w_rf_grouped, w_rf_rows, half, on_scalar=half == 0)
        consumed(RF)
        grouped = new_grouped()
        regroup_words(grouped, loaded_rf[0], 0, on_scalar=True)
        quantise(w_rf_grouped, w_codes[RF][:], w_scales[RF][:])
        regroup_words(grouped, loaded_rf[0], 1)
        consumed(RF)
        quantise_block(grouped, RF, 0)
        bias_bank = work.tile([P, P], BF16, tag="work")
        nc.tensor.transpose(bias_bank[:], bias_rows[:], ident_bf16[:])
        bias_pos = const.tile([P, 2 * CHUNKS], F32)
        bias_neg = const.tile([P, 2 * CHUNKS], F32)
        nc.vector.tensor_scalar(
            out=bias_neg[:], in0=bias_bank[:, 0 : 2 * CHUNKS], scalar1=-1.0, scalar2=None, op0=ALU.mult
        )
        nc.vector.tensor_copy(out=bias_pos[:], in_=bias_bank[:, 0 : 2 * CHUNKS])

        first = BATCHES[0]
        for n, (br, blk) in enumerate(first):
            if n + 1 < len(first):
                if first[n + 1] == (BB, 0):
                    grouped = new_grouped()
                    for half in range(2):
                        regroup_words(grouped, loaded_rf["weights"], half, on_scalar=half < WBB_S)
                    quantise(grouped, w_codes[BB][:], w_scales[BB][:])
                    consumed(RF)
                prepare(*first[n + 1])
            for pair in range(PAIRS):
                sigmoid_tile(br, blk, pair)

        def tiles_of(batch):
            return sorted(((br, blk, pair) for br, blk in batch for pair in range(PAIRS)), key=lambda x: (x[1], x[2], x[0]))

        multiplied = []
        returned = set()

        def multiply(tile, scalar_helps=False):
            if tile is not None:
                mish_tile(*tile)
            multiplied.append(tile)
            if len(multiplied) > BEHIND and multiplied[-1 - BEHIND] is not None:
                br, blk, pair = multiplied[-1 - BEHIND]
                ready = multiplied[: len(multiplied) - BEHIND]
                if (blk, pair) not in returned and all((b, blk, pair) in ready for b in BRANCHES):
                    returned.add((blk, pair))
                    way_back(blk, pair, scalar_helps, chunkwise=(blk, pair) == (BLOCKS - 1, PAIRS - 1))

        beats = []
        later = []

        def beat(count):
            beats.append(0)
            for n in range(count):
                if pieces:
                    run_piece()
            for entry in list(later):
                if entry[0] <= len(beats):
                    later.remove(entry)
                    entry[1](*entry[2])

        def start_division(blk, pair):
            divide_before(blk, pair)
            now = len(beats)
            for n in range(4):
                later.append((now + DIVIDE_AFTER + n, divide, (blk, pair, slice(n * P, (n + 1) * P))))
            later.append((now + DIVIDE_AFTER + 4, finish_division, (blk, pair)))

        def start_divisions(*here):
            for q, place in DIVIDED.items():
                if place == here:
                    start_division(*q)

        def finish_division(blk, pair):
            add_loaded()
            divide_after(blk, pair)
            now = len(beats)
            for br in BRANCHES:
                later.append((now + MULTIPLY_AFTER + 2 * br, multiply, ((br, blk, pair),)))

        waiting = []
        for b, batch in enumerate(BATCHES):
            last = b + 1 == len(BATCHES)
            tiles = [t for t in tiles_of(batch) if (t[1], t[2]) not in DIVIDED]
            following = () if last else BATCHES[b + 1]
            sigmoids = [(br, blk, pair) for br, blk in following for pair in range(PAIRS)]
            add_loaded()
            for unit in following:
                queue_unit(*unit)
            for n, tile in enumerate(tiles):
                log_tile(*tile)
                start_divisions(b, 0, n)
                beat(LOG_PIECES[n % len(LOG_PIECES)])
                for k in range(EXTRA_LN):
                    if pieces:
                        run_piece()
                if waiting and n >= 1:
                    multiply(waiting.pop(0), scalar_helps=last and LN_HELPS)
            woven = 0
            for n, tile in enumerate(tiles):
                while woven < len(sigmoids) and woven * len(tiles) <= n * len(sigmoids):
                    ensure(sigmoids[woven][:2])
                    sigmoid_tile(*sigmoids[woven])
                    woven += 1
                    beat(P_SIG)
                start_divisions(b, 1, n)
                tanh_tile(*tile, pieces=PAIR if last and n == len(tiles) - 1 else 1)
                waiting.append(tile)
                while len(waiting) > (TAIL_LAG if last else LAG):
                    multiply(waiting.pop(0), scalar_helps=last and n >= len(tiles) - TAIL_HELP)
                beat(P_TANH)
            for tile in sigmoids[woven:]:
                ensure(tile[:2])
                sigmoid_tile(*tile)
                beat(2)
        while waiting:
            multiply(waiting.pop(0), scalar_helps=True)
        while later:
            beat(2)
        for n in range(BEHIND):
            multiply(None, scalar_helps=True)
